import numpy as np
import ml_dtypes


def mxq(x, axis, fmt="e4m3"):
    dtype, down = {"e4m3": (ml_dtypes.float8_e4m3fn, 7), "e5m2": (ml_dtypes.float8_e5m2, 14)}[fmt]
    v = np.moveaxis(np.asarray(x, np.float32).astype(ml_dtypes.bfloat16).astype(np.float64), axis, -1)
    blocks = v.reshape(v.shape[:-1] + (-1, 32))
    amax = np.abs(blocks).max(-1, keepdims=True)
    byte = np.maximum(np.where(amax > 0, np.frexp(amax)[1] - 1 + 127, 0) - down, 1)
    scale = np.exp2(byte - 127.0)
    codes = (blocks / scale).astype(np.float32).astype(dtype).astype(np.float64)
    return np.moveaxis((codes * scale).reshape(v.shape), -1, axis)


WIDE = False


def mx_kscale(k):
    if not WIDE:
        return np.ones(k)
    levels = np.array([10, -10, 5, -5, 0])
    a = np.random.permutation(np.resize(levels, k // 512 * 4)).reshape(k // 512, 4)
    idx = np.arange(k)
    return np.exp2(a[idx // 512, idx % 128 // 32])


BF16 = ml_dtypes.bfloat16


def bf(x):
    return np.asarray(x, np.float32).astype(BF16)


def f64(x):
    return np.asarray(x).astype(np.float64)


E2M1 = np.array([0.0, 0.5, 1.0, 1.5, 2.0, 3.0, 4.0, 6.0, -0.0, -0.5, -1.0, -1.5, -2.0, -3.0, -4.0, -6.0])


def pack_weight(w, fmt):
    k, n = w.shape
    w = f64(bf(w)).reshape(k // 32, 32, n)
    amax = np.abs(w).max(1)
    if fmt == "e4m3":
        byte = np.frexp(amax)[1] - 1 + 127 - 7
    else:
        mant, ex = np.frexp(amax / 6.0)
        byte = np.where(mant > 0.5, ex, ex - 1) + 127
    byte = np.clip(np.where(amax > 0, byte, 1), 1, 254)
    scaled = (w * np.exp2(127.0 - byte)[:, None, :]).reshape(k, n).astype(np.float32)
    by_word = np.ascontiguousarray(scaled.reshape(k // 512, 128, 4, n).transpose(0, 1, 3, 2))
    if fmt == "e4m3":
        words = by_word.astype(ml_dtypes.float8_e4m3fn).view(np.uint8)
    else:
        c = by_word.astype(ml_dtypes.float4_e2m1fn).view(np.uint8) & 0xF
        words = c[..., 0::2] | (c[..., 1::2] << 4)
    return np.ascontiguousarray(words), np.ascontiguousarray(byte.astype(np.uint8).reshape(k // 512, 16, n))


def unpack_weight(words, scales, fmt):
    g, p, n, _ = words.shape
    if fmt == "e4m3":
        vals = np.ascontiguousarray(words).view(ml_dtypes.float8_e4m3fn).astype(np.float64)
    else:
        nib = np.empty((g, p, n, 4), np.uint8)
        nib[..., 0::2] = words & 0xF
        nib[..., 1::2] = words >> 4
        vals = E2M1[nib]
    vals = vals * np.repeat(np.exp2(scales.astype(np.float64) - 127.0), 8, axis=1)[..., None]
    return vals.transpose(0, 1, 3, 2).reshape(g * 512, n)


B, N, CIN, COUT = 4, 512, 512, 256
NW = 2


def xavier():
    return np.random.uniform(-1.0, 1.0, (CIN, COUT)) * (1.414 * np.sqrt(6.0 / (CIN + COUT)))


def setup_inputs():
    s = mx_kscale(CIN)
    x = bf(np.random.standard_normal((B, N, CIN)) * s)
    stack = np.stack([xavier(), xavier()]) / s[None, :, None]
    W_words, W_scales = pack_weight(stack.reshape(-1, COUT), "e4m3")
    return {"x": x,
            "W_words": W_words,
            "W_scales": W_scales,
            "M": bf(1.0 + 0.1 * np.random.standard_normal((N, COUT))),
            "adj": bf(np.random.uniform(0.0, 1.0, (N, N)) * 1.5 / np.sqrt(N) + np.eye(N) * np.random.uniform(0.5, 1.5, (N, 1))),
            "adj2": bf(np.random.standard_normal((N, N)) * 0.5 / np.sqrt(N)),
            "bias": bf(np.random.standard_normal(COUT) * 0.5)}


def reference(x, W_words, W_scales, M, adj, adj2, bias):
    xq = mxq(f64(x), 2, "e4m3")
    Wf = unpack_weight(W_words, W_scales, "e4m3").reshape(NW, CIN, COUT)
    h0 = xq @ Wf[0]
    h1 = xq @ Wf[1]
    A = f64(adj) + f64(adj2)
    A = (A.T + A) * 0.5
    E = np.eye(N)
    a_self = np.diagonal(A)
    a_off = A * (1.0 - E)
    g0 = f64(M) * h0
    g1 = f64(M) * h1
    agg = mxq(a_off, 1, "e4m3") @ mxq(g1, 1, "e4m3")
    return a_self[None, :, None] * g0 + agg + f64(bias)

@@ -1,0 +1,230 @@
+from contextlib import ExitStack
+
+import concourse.mybir as mybir
+from concourse.masks import make_identity
+
+FP8X4 = mybir.dt.float8_e4m3fn_x4
+BF16 = mybir.dt.bfloat16
+F32 = mybir.dt.float32
+I32 = mybir.dt.int32
+U32 = mybir.dt.uint32
+U8 = mybir.dt.uint8
+ALU = mybir.AluOpType
+ACT = mybir.ActivationFunctionType
+
+P = 128
+PACK = 4
+BATCH, NODES, CIN, COUT = 4, 512, 512, 256
+HALVES = COUT // P
+BANK = 512
+
+FLOPS = 2 * BATCH * NODES * CIN * 2 * COUT + 2 * BATCH * NODES * NODES * COUT
+
+
+def tile_modulatedgraphconv_pa_e_kernel(tc, x, W_words, W_scales, M, adj, adj2, bias, out):
+    nc = tc.nc
+    with ExitStack() as ctx:
+        keep = ctx.enter_context(tc.tile_pool(name="keep", bufs=1))
+        work = ctx.enter_context(tc.tile_pool(name="work", bufs=2))
+        psum = ctx.enter_context(tc.psum_pool(name="psum", bufs=2))
+
+        w_scales = keep.tile([P, 2 * COUT], U8, align_bytes=64)
+        nc.vector.memset(w_scales[:].bitcast(I32), 0)
+        for quadrant in range(4):
+            nc.sync.dma_start(
+                out=w_scales[32 * quadrant : 32 * quadrant + 4, :].bitcast(I32).rearrange("r (e n) -> r e n", e=2),
+                in_=W_scales[:, 4 * quadrant : 4 * quadrant + 4, :].rearrange("e r n -> r e n").bitcast(I32),
+            )
+        bias_rows = keep.tile([P, P], BF16)
+        nc.vector.memset(bias_rows[:], 0.0)
+        nc.sync.dma_start(out=bias_rows[0:HALVES, :], in_=bias.rearrange("(h c) -> h c", h=HALVES))
+
+        x_sb = [keep.tile([P, PACK, CIN], BF16, name="x_sb%d" % b) for b in range(BATCH)]
+        w_words = keep.tile([P, 2 * COUT], U32, align_bytes=64)
+        m_sb = keep.tile([P, PACK, COUT], BF16)
+        adj_sb = keep.tile([P, PACK, NODES], BF16)
+        adj2_sb = keep.tile([P, PACK, NODES], BF16)
+        nc.sync.dma_start(out=x_sb[0][:], in_=x[0].rearrange("(p t) k -> p t k", t=PACK))
+        nc.sync.dma_start(
+            out=w_words[:].bitcast(I32).rearrange("p (e n) -> p e n", e=2),
+            in_=W_words.rearrange("e p n t -> p e (n t)").bitcast(I32),
+        )
+        nc.sync.dma_start(out=m_sb[:], in_=M.rearrange("(p t) c -> p t c", t=PACK))
+        nc.sync.dma_start(out=adj_sb[:], in_=adj.rearrange("(p t) i -> p t i", t=PACK))
+        nc.sync.dma_start(out=adj2_sb[:], in_=adj2.rearrange("(p t) i -> p t i", t=PACK))
+        for b in range(1, BATCH):
+            nc.sync.dma_start(out=x_sb[b][:], in_=x[b].rearrange("(p t) k -> p t k", t=PACK))
+
+        ident_f32 = keep.tile([P, P], F32)
+        make_identity(nc, ident_f32[:])
+        ident_bf16 = keep.tile([P, P], BF16)
+        nc.vector.tensor_copy(out=ident_bf16[:], in_=ident_f32[:])
+        twice_ident = keep.tile([P, P], F32)
+        nc.vector.tensor_scalar(out=twice_ident[:], in0=ident_f32[:], scalar1=2.0, scalar2=None, op0=ALU.mult)
+        off_diagonal = keep.tile([P, P], F32)
+        nc.vector.tensor_scalar(
+            out=off_diagonal[:], in0=ident_f32[:], scalar1=-1.0, scalar2=1.0, op0=ALU.mult, op1=ALU.add
+        )
+
+        bias_ps = psum.tile([P, P], BF16, tag="back")
+        nc.tensor.transpose(bias_ps[:], bias_rows[:], ident_bf16[:])
+        bias_col = keep.tile([P, HALVES], F32)
+        nc.scalar.copy(out=bias_col[:], in_=bias_ps[:, 0:HALVES])
+
+        xq_words = keep.tile([P, BATCH, NODES], U32, align_bytes=64)
+        xq_scales = keep.tile([P, BATCH, NODES], U8, align_bytes=64)
+        g_words = keep.tile([P, BATCH, COUT], U32, align_bytes=64)
+        g_scales = keep.tile([P, BATCH, COUT], U8, align_bytes=64)
+        a_words = keep.tile([P, NODES], U32, align_bytes=64)
+        a_scales = keep.tile([P, NODES], U8, align_bytes=64)
+        gain_t = keep.tile([P, HALVES, NODES], F32)
+
+        def project(b):
+            x_pairs = x_sb[b][:].rearrange("p t k -> p (t k)").bitcast(F32)
+            x_pairs = x_pairs.rearrange("p (t w u) -> p t w u", t=PACK, u=2)
+            x_grouped = work.tile([P, NODES * PACK], BF16, align_bytes=64)
+            x_grouped_pairs = x_grouped[:].bitcast(F32).rearrange("p (s r u) -> p s r u", s=PACK, u=2)
+            for first_slot in range(0, PACK, 2):
+                xt_ps = psum.tile([P, 2, 2, P], F32, tag="xt")
+                for s in range(2):
+                    for u in range(2):
+                        nc.tensor.transpose(xt_ps[:, s, u, :], x_pairs[:, first_slot + s, :, u], ident_f32[:])
+                nc.scalar.copy(
+                    out=x_grouped_pairs[:, first_slot : first_slot + 2, :, :],
+                    in_=xt_ps[:].rearrange("p s u r -> p s r u"),
+                )
+            nc.vector.quantize_mx(
+                out=xq_words[:, b, :].bitcast(FP8X4), scales=xq_scales[:, b, :], in_=x_grouped[:]
+            )
+
+            g_grouped = work.tile([P, COUT, PACK], BF16, align_bytes=64)
+            for h in range(HALVES):
+                channels = slice(h * P, (h + 1) * P)
+                w1_cols = slice(COUT + h * P, COUT + (h + 1) * P)
+                h1_ps = psum.tile([P, PACK, P], F32, tag="h1")
+                for t in range(PACK):
+                    nodes = slice(t * P, (t + 1) * P)
+                    nc.tensor.matmul_mx(
+                        out=h1_ps[:, t, :],
+                        lhsT=xq_words[:, b, nodes].bitcast(FP8X4),
+                        lhsT_scale=xq_scales[:, b, nodes],
+                        rhs=w_words[:, w1_cols].bitcast(FP8X4),
+                        rhs_scale=w_scales[:, w1_cols],
+                        start=True,
+                        stop=True,
+                    )
+                nc.vector.tensor_tensor(
+                    out=g_grouped[:, channels, :],
+                    in0=h1_ps[:].rearrange("p t c -> p c t"),
+                    in1=m_sb[:, :, channels].rearrange("p t c -> p c t"),
+                    op=ALU.mult,
+                )
+            nc.vector.quantize_mx(
+                out=g_words[:, b, :].bitcast(FP8X4),
+                scales=g_scales[:, b, :],
+                in_=g_grouped[:].rearrange("p c t -> p (c t)"),
+            )
+
+        def adjacency():
+            half_s = keep.tile([P, PACK, PACK, P], F32)
+            for r in range(PACK):
+                s_ps = psum.tile([P, BANK], F32, tag="back")
+                nc.tensor.matmul(out=s_ps[:], lhsT=ident_bf16[:], rhs=adj_sb[:, r, :], start=True, stop=False)
+                nc.tensor.matmul(out=s_ps[:], lhsT=ident_bf16[:], rhs=adj2_sb[:, r, :], start=False, stop=True)
+                nc.scalar.mul(out=half_s[:, r, :, :], in_=s_ps[:].rearrange("p (q c) -> p c q", c=PACK), mul=0.5)
+
+            diag_blocks = half_s[:].rearrange("p r c q -> p (r c) q")[:, 0 : PACK * PACK : PACK + 1, :]
+            diag_only = keep.tile([P, PACK, P], F32)
+            nc.gpsimd.tensor_tensor(
+                out=diag_only[:],
+                in0=diag_blocks,
+                in1=twice_ident[:].unsqueeze(1).to_broadcast([P, PACK, P]),
+                op=ALU.mult,
+            )
+            nc.gpsimd.tensor_tensor(
+                out=diag_blocks,
+                in0=diag_blocks,
+                in1=off_diagonal[:].unsqueeze(1).to_broadcast([P, PACK, P]),
+                op=ALU.mult,
+            )
+            a_self = keep.tile([P, PACK], F32)
+            gain = keep.tile([P, PACK, COUT], F32)
+            for t in range(PACK):
+                nc.scalar.activation(
+                    out=diag_only[:, t, :], in_=diag_only[:, t, :], func=ACT.Copy, accum_out=a_self[:, t : t + 1]
+                )
+            for t in range(PACK):
+                nc.scalar.activation(out=gain[:, t, :], in_=m_sb[:, t, :], func=ACT.Copy, scale=a_self[:, t : t + 1])
+            for h in range(HALVES):
+                gain_ps = psum.tile([P, PACK, P], F32, tag="back")
+                for t in range(PACK):
+                    nc.tensor.transpose(gain_ps[:, t, :], gain[:, t, h * P : (h + 1) * P], ident_f32[:])
+                nc.scalar.copy(out=gain_t[:, h, :], in_=gain_ps[:].rearrange("p t r -> p (t r)"))
+
+            a_grouped = keep.tile([P, PACK, P, PACK], BF16, align_bytes=64)
+            for c in range(PACK):
+                st_ps = psum.tile([P, PACK, P], F32, tag="ct")
+                for t in range(PACK):
+                    nc.tensor.transpose(st_ps[:, t, :], half_s[:, c, t, :], ident_f32[:])
+                nc.vector.tensor_tensor(
+                    out=a_grouped[:, c, :, :],
+                    in0=st_ps[:].rearrange("p t q -> p q t"),
+                    in1=half_s[:, :, c, :].rearrange("p t q -> p q t"),
+                    op=ALU.add,
+                )
+            nc.vector.quantize_mx(
+                out=a_words[:].bitcast(FP8X4),
+                scales=a_scales[:],
+                in_=a_grouped[:].rearrange("p c q t -> p (c q t)"),
+            )
+
+        def combine(b):
+            out_t = work.tile([P, HALVES, NODES], F32)
+            for h in range(HALVES):
+                channels = slice(h * P, (h + 1) * P)
+                h0t_ps = psum.tile([P, BANK], F32, tag="ct")
+                nc.tensor.matmul_mx(
+                    out=h0t_ps[:],
+                    lhsT=w_words[:, channels].bitcast(FP8X4),
+                    lhsT_scale=w_scales[:, channels],
+                    rhs=xq_words[:, b, :].bitcast(FP8X4),
+                    rhs_scale=xq_scales[:, b, :],
+                    start=True,
+                    stop=True,
+                )
+                self_t = work.tile([P, NODES], F32)
+                nc.vector.tensor_tensor(out=self_t[:], in0=h0t_ps[:], in1=gain_t[:, h, :], op=ALU.mult)
+                agg_ps = psum.tile([P, BANK], F32, tag="ct")
+                nc.tensor.matmul_mx(
+                    out=agg_ps[:],
+                    lhsT=g_words[:, b, channels].bitcast(FP8X4),
+                    lhsT_scale=g_scales[:, b, channels],
+                    rhs=a_words[:].bitcast(FP8X4),
+                    rhs_scale=a_scales[:],
+                    start=True,
+                    stop=True,
+                )
+                nc.vector.scalar_tensor_tensor(
+                    out=out_t[:, h, :],
+                    in0=agg_ps[:],
+                    scalar=bias_col[:, h : h + 1],
+                    in1=self_t[:],
+                    op0=ALU.add,
+                    op1=ALU.add,
+                )
+            out_sb = work.tile([P, PACK, COUT], F32)
+            for first_slot in range(0, PACK, 2):
+                back_ps = psum.tile([P, 2, COUT], F32, tag="back")
+                for s in range(2):
+                    nodes = slice((first_slot + s) * P, (first_slot + s + 1) * P)
+                    for h in range(HALVES):
+                        nc.tensor.transpose(back_ps[:, s, h * P : (h + 1) * P], out_t[:, h, nodes], ident_f32[:])
+                nc.scalar.copy(out=out_sb[:, first_slot : first_slot + 2, :], in_=back_ps[:])
+            nc.sync.dma_start(out=out[b].rearrange("(p t) c -> p t c", t=PACK), in_=out_sb[:])
+
+        project(0)
+        adjacency()
+        for b in range(1, BATCH):
+            project(b)
+            combine(b - 1)
+        combine(BATCH - 1)

@@ -25,51 +25,58 @@ def tile_modulatedgraphconv_pa_e_kernel(tc, x, W_words, W_scales, M, adj, adj2, 
     nc = tc.nc
     with ExitStack() as ctx:
         keep = ctx.enter_context(tc.tile_pool(name="keep", bufs=1))
-        work = ctx.enter_context(tc.tile_pool(name="work", bufs=2))
-        psum = ctx.enter_context(tc.psum_pool(name="psum", bufs=2))
+        per_batch = ctx.enter_context(tc.tile_pool(name="per_batch", bufs=BATCH))
+        psum = ctx.enter_context(tc.psum_pool(name="psum", bufs=1))
 
+        def bank_for_scalar(shape, dtype=F32):
+            return psum.tile(shape, dtype, name="bank_for_scalar", tag="for_scalar", bufs=3)
+
+        def bank_for_vector(shape):
+            return psum.tile(shape, F32, name="bank_for_vector", tag="for_vector", bufs=5)
+
+        ctx.enter_context(tc.manual_schedule())
+
+        x_sb = [keep.tile([P, PACK, CIN], BF16, name="x_sb%d" % b) for b in range(BATCH)]
+        w_words = keep.tile([P, 2 * COUT], U32, align_bytes=64)
         w_scales = keep.tile([P, 2 * COUT], U8, align_bytes=64)
+        m_sb = keep.tile([P, PACK, COUT], BF16)
+        bias_rows = keep.tile([P, P], BF16)
+        adj_sb = keep.tile([P, PACK, NODES], BF16)
+        adj2_sb = keep.tile([P, PACK, NODES], BF16)
+
+        def load_x(b):
+            nc.sync.dma_start(out=x_sb[b][:], in_=x[b].rearrange("(p t) k -> p t k", t=PACK))
+
+        load_x(0)
+        load_x(1)
+        nc.sync.dma_start(
+            out=w_words[:].bitcast(I32).rearrange("p (e n) -> p e n", e=2),
+            in_=W_words.rearrange("e p n t -> p e (n t)").bitcast(I32),
+        )
         nc.vector.memset(w_scales[:].bitcast(I32), 0)
         for quadrant in range(4):
             nc.sync.dma_start(
                 out=w_scales[32 * quadrant : 32 * quadrant + 4, :].bitcast(I32).rearrange("r (e n) -> r e n", e=2),
                 in_=W_scales[:, 4 * quadrant : 4 * quadrant + 4, :].rearrange("e r n -> r e n").bitcast(I32),
             )
-        bias_rows = keep.tile([P, P], BF16)
-        nc.vector.memset(bias_rows[:], 0.0)
-        nc.sync.dma_start(out=bias_rows[0:HALVES, :], in_=bias.rearrange("(h c) -> h c", h=HALVES))
-
-        x_sb = [keep.tile([P, PACK, CIN], BF16, name="x_sb%d" % b) for b in range(BATCH)]
-        w_words = keep.tile([P, 2 * COUT], U32, align_bytes=64)
-        m_sb = keep.tile([P, PACK, COUT], BF16)
-        adj_sb = keep.tile([P, PACK, NODES], BF16)
-        adj2_sb = keep.tile([P, PACK, NODES], BF16)
-        nc.sync.dma_start(out=x_sb[0][:], in_=x[0].rearrange("(p t) k -> p t k", t=PACK))
-        nc.sync.dma_start(
-            out=w_words[:].bitcast(I32).rearrange("p (e n) -> p e n", e=2),
-            in_=W_words.rearrange("e p n t -> p e (n t)").bitcast(I32),
-        )
         nc.sync.dma_start(out=m_sb[:], in_=M.rearrange("(p t) c -> p t c", t=PACK))
+        load_x(2)
+        load_x(3)
         nc.sync.dma_start(out=adj_sb[:], in_=adj.rearrange("(p t) i -> p t i", t=PACK))
         nc.sync.dma_start(out=adj2_sb[:], in_=adj2.rearrange("(p t) i -> p t i", t=PACK))
-        for b in range(1, BATCH):
-            nc.sync.dma_start(out=x_sb[b][:], in_=x[b].rearrange("(p t) k -> p t k", t=PACK))
+        nc.vector.memset(bias_rows[:], 0.0)
+        nc.sync.dma_start(out=bias_rows[0:HALVES, :], in_=bias.rearrange("(h c) -> h c", h=HALVES))
 
         ident_f32 = keep.tile([P, P], F32)
         make_identity(nc, ident_f32[:])
         ident_bf16 = keep.tile([P, P], BF16)
         nc.vector.tensor_copy(out=ident_bf16[:], in_=ident_f32[:])
-        twice_ident = keep.tile([P, P], F32)
-        nc.vector.tensor_scalar(out=twice_ident[:], in0=ident_f32[:], scalar1=2.0, scalar2=None, op0=ALU.mult)
         off_diagonal = keep.tile([P, P], F32)
         nc.vector.tensor_scalar(
             out=off_diagonal[:], in0=ident_f32[:], scalar1=-1.0, scalar2=1.0, op0=ALU.mult, op1=ALU.add
         )
-
-        bias_ps = psum.tile([P, P], BF16, tag="back")
-        nc.tensor.transpose(bias_ps[:], bias_rows[:], ident_bf16[:])
-        bias_col = keep.tile([P, HALVES], F32)
-        nc.scalar.copy(out=bias_col[:], in_=bias_ps[:, 0:HALVES])
+        twice_ident = keep.tile([P, P], F32)
+        nc.scalar.mul(out=twice_ident[:], in_=ident_f32[:], mul=2.0)
 
         xq_words = keep.tile([P, BATCH, NODES], U32, align_bytes=64)
         xq_scales = keep.tile([P, BATCH, NODES], U8, align_bytes=64)
@@ -77,35 +84,39 @@ def tile_modulatedgraphconv_pa_e_kernel(tc, x, W_words, W_scales, M, adj, adj2, 
         g_scales = keep.tile([P, BATCH, COUT], U8, align_bytes=64)
         a_words = keep.tile([P, NODES], U32, align_bytes=64)
         a_scales = keep.tile([P, NODES], U8, align_bytes=64)
-        gain_t = keep.tile([P, HALVES, NODES], F32)
 
-        def project(b):
+        x_grouped = {}
+        h1_banks = {}
+        g_grouped = {}
+
+        def transpose_x(b):
             x_pairs = x_sb[b][:].rearrange("p t k -> p (t k)").bitcast(F32)
             x_pairs = x_pairs.rearrange("p (t w u) -> p t w u", t=PACK, u=2)
-            x_grouped = work.tile([P, NODES * PACK], BF16, align_bytes=64)
-            x_grouped_pairs = x_grouped[:].bitcast(F32).rearrange("p (s r u) -> p s r u", s=PACK, u=2)
+            x_grouped[b] = per_batch.tile([P, NODES * PACK], BF16, name="x_grouped", align_bytes=64)
+            grouped_pairs = x_grouped[b][:].bitcast(F32).rearrange("p (s r u) -> p s r u", s=PACK, u=2)
             for first_slot in range(0, PACK, 2):
-                xt_ps = psum.tile([P, 2, 2, P], F32, tag="xt")
+                xt_ps = bank_for_scalar([P, 2, 2, P])
                 for s in range(2):
                     for u in range(2):
                         nc.tensor.transpose(xt_ps[:, s, u, :], x_pairs[:, first_slot + s, :, u], ident_f32[:])
                 nc.scalar.copy(
-                    out=x_grouped_pairs[:, first_slot : first_slot + 2, :, :],
+                    out=grouped_pairs[:, first_slot : first_slot + 2, :, :],
                     in_=xt_ps[:].rearrange("p s u r -> p s r u"),
                 )
+
+        def quantise_x(b):
             nc.vector.quantize_mx(
-                out=xq_words[:, b, :].bitcast(FP8X4), scales=xq_scales[:, b, :], in_=x_grouped[:]
+                out=xq_words[:, b, :].bitcast(FP8X4), scales=xq_scales[:, b, :], in_=x_grouped[b][:]
             )
 
-            g_grouped = work.tile([P, COUT, PACK], BF16, align_bytes=64)
+        def project_h1(b):
             for h in range(HALVES):
-                channels = slice(h * P, (h + 1) * P)
                 w1_cols = slice(COUT + h * P, COUT + (h + 1) * P)
-                h1_ps = psum.tile([P, PACK, P], F32, tag="h1")
+                h1_banks[(b, h)] = bank_for_vector([P, PACK, P])
                 for t in range(PACK):
                     nodes = slice(t * P, (t + 1) * P)
                     nc.tensor.matmul_mx(
-                        out=h1_ps[:, t, :],
+                        out=h1_banks[(b, h)][:, t, :],
                         lhsT=xq_words[:, b, nodes].bitcast(FP8X4),
                         lhsT_scale=xq_scales[:, b, nodes],
                         rhs=w_words[:, w1_cols].bitcast(FP8X4),
@@ -113,57 +124,57 @@ def tile_modulatedgraphconv_pa_e_kernel(tc, x, W_words, W_scales, M, adj, adj2, 
                         start=True,
                         stop=True,
                     )
-                nc.vector.tensor_tensor(
-                    out=g_grouped[:, channels, :],
-                    in0=h1_ps[:].rearrange("p t c -> p c t"),
-                    in1=m_sb[:, :, channels].rearrange("p t c -> p c t"),
-                    op=ALU.mult,
-                )
+
+        def modulate(b, h):
+            if h == 0:
+                g_grouped[b] = per_batch.tile([P, COUT, PACK], BF16, name="g_grouped", align_bytes=64)
+            channels = slice(h * P, (h + 1) * P)
+            nc.vector.tensor_tensor(
+                out=g_grouped[b][:, channels, :],
+                in0=h1_banks[(b, h)][:].rearrange("p t c -> p c t"),
+                in1=m_sb[:, :, channels].rearrange("p t c -> p c t"),
+                op=ALU.mult,
+            )
+
+        def quantise_g(b):
             nc.vector.quantize_mx(
                 out=g_words[:, b, :].bitcast(FP8X4),
                 scales=g_scales[:, b, :],
-                in_=g_grouped[:].rearrange("p c t -> p (c t)"),
+                in_=g_grouped[b][:].rearrange("p c t -> p (c t)"),
             )
 
-        def adjacency():
-            half_s = keep.tile([P, PACK, PACK, P], F32)
-            for r in range(PACK):
-                s_ps = psum.tile([P, BANK], F32, tag="back")
-                nc.tensor.matmul(out=s_ps[:], lhsT=ident_bf16[:], rhs=adj_sb[:, r, :], start=True, stop=False)
-                nc.tensor.matmul(out=s_ps[:], lhsT=ident_bf16[:], rhs=adj2_sb[:, r, :], start=False, stop=True)
-                nc.scalar.mul(out=half_s[:, r, :, :], in_=s_ps[:].rearrange("p (q c) -> p c q", c=PACK), mul=0.5)
+        half_s = keep.tile([P, PACK, PACK, P], F32)
+        diag_only = keep.tile([P, PACK, P], F32)
 
-            diag_blocks = half_s[:].rearrange("p r c q -> p (r c) q")[:, 0 : PACK * PACK : PACK + 1, :]
-            diag_only = keep.tile([P, PACK, P], F32)
-            nc.gpsimd.tensor_tensor(
-                out=diag_only[:],
-                in0=diag_blocks,
-                in1=twice_ident[:].unsqueeze(1).to_broadcast([P, PACK, P]),
-                op=ALU.mult,
-            )
-            nc.gpsimd.tensor_tensor(
-                out=diag_blocks,
-                in0=diag_blocks,
-                in1=off_diagonal[:].unsqueeze(1).to_broadcast([P, PACK, P]),
-                op=ALU.mult,
-            )
-            a_self = keep.tile([P, PACK], F32)
-            gain = keep.tile([P, PACK, COUT], F32)
+        def add_adjacency(r):
+            s_ps = bank_for_scalar([P, BANK])
+            nc.tensor.matmul(out=s_ps[:], lhsT=ident_bf16[:], rhs=adj_sb[:, r, :], start=True, stop=False)
+            nc.tensor.matmul(out=s_ps[:], lhsT=ident_bf16[:], rhs=adj2_sb[:, r, :], start=False, stop=True)
+            nc.scalar.mul(out=half_s[:, r, :, :], in_=s_ps[:].rearrange("p (q c) -> p c q", c=PACK), mul=0.5)
+            nc.gpsimd.tensor_tensor(out=diag_only[:, r, :], in0=half_s[:, r, r, :], in1=twice_ident[:], op=ALU.mult)
+            nc.gpsimd.tensor_tensor(out=half_s[:, r, r, :], in0=half_s[:, r, r, :], in1=off_diagonal[:], op=ALU.mult)
+
+        a_self = keep.tile([P, PACK], F32)
+        gain = keep.tile([P, PACK, COUT], F32)
+        bias_col = keep.tile([P, HALVES], F32)
+
+        def self_gain():
             for t in range(PACK):
                 nc.scalar.activation(
                     out=diag_only[:, t, :], in_=diag_only[:, t, :], func=ACT.Copy, accum_out=a_self[:, t : t + 1]
                 )
             for t in range(PACK):
                 nc.scalar.activation(out=gain[:, t, :], in_=m_sb[:, t, :], func=ACT.Copy, scale=a_self[:, t : t + 1])
-            for h in range(HALVES):
-                gain_ps = psum.tile([P, PACK, P], F32, tag="back")
-                for t in range(PACK):
-                    nc.tensor.transpose(gain_ps[:, t, :], gain[:, t, h * P : (h + 1) * P], ident_f32[:])
-                nc.scalar.copy(out=gain_t[:, h, :], in_=gain_ps[:].rearrange("p t r -> p (t r)"))
 
+        def bias_onto_partitions():
+            bias_ps = bank_for_scalar([P, P], BF16)
+            nc.tensor.transpose(bias_ps[:], bias_rows[:], ident_bf16[:])
+            nc.scalar.copy(out=bias_col[:], in_=bias_ps[:, 0:HALVES])
+
+        def symmetrise():
             a_grouped = keep.tile([P, PACK, P, PACK], BF16, align_bytes=64)
             for c in range(PACK):
-                st_ps = psum.tile([P, PACK, P], F32, tag="ct")
+                st_ps = bank_for_vector([P, PACK, P])
                 for t in range(PACK):
                     nc.tensor.transpose(st_ps[:, t, :], half_s[:, c, t, :], ident_f32[:])
                 nc.vector.tensor_tensor(
@@ -178,23 +189,32 @@ def tile_modulatedgraphconv_pa_e_kernel(tc, x, W_words, W_scales, M, adj, adj2, 
                 in_=a_grouped[:].rearrange("p c q t -> p (c q t)"),
             )
 
-        def combine(b):
-            out_t = work.tile([P, HALVES, NODES], F32)
+        self_term = {}
+        agg_t = {}
+
+        def weigh_self(b):
+            self_term[b] = per_batch.tile([P, PACK, COUT], F32, name="self_term")
+            for first_slot in range(0, PACK, 2):
+                h0_ps = bank_for_vector([P, 2, COUT])
+                for s in range(2):
+                    nodes = slice((first_slot + s) * P, (first_slot + s + 1) * P)
+                    nc.tensor.matmul_mx(
+                        out=h0_ps[:, s, :],
+                        lhsT=xq_words[:, b, nodes].bitcast(FP8X4),
+                        lhsT_scale=xq_scales[:, b, nodes],
+                        rhs=w_words[:, 0:COUT].bitcast(FP8X4),
+                        rhs_scale=w_scales[:, 0:COUT],
+                        start=True,
+                        stop=True,
+                    )
+                slots = slice(first_slot, first_slot + 2)
+                nc.vector.tensor_tensor(out=self_term[b][:, slots, :], in0=h0_ps[:], in1=gain[:, slots, :], op=ALU.mult)
+
+        def aggregate(b):
+            agg_t[b] = per_batch.tile([P, HALVES, NODES], F32, name="agg_t")
             for h in range(HALVES):
                 channels = slice(h * P, (h + 1) * P)
-                h0t_ps = psum.tile([P, BANK], F32, tag="ct")
-                nc.tensor.matmul_mx(
-                    out=h0t_ps[:],
-                    lhsT=w_words[:, channels].bitcast(FP8X4),
-                    lhsT_scale=w_scales[:, channels],
-                    rhs=xq_words[:, b, :].bitcast(FP8X4),
-                    rhs_scale=xq_scales[:, b, :],
-                    start=True,
-                    stop=True,
-                )
-                self_t = work.tile([P, NODES], F32)
-                nc.vector.tensor_tensor(out=self_t[:], in0=h0t_ps[:], in1=gain_t[:, h, :], op=ALU.mult)
-                agg_ps = psum.tile([P, BANK], F32, tag="ct")
+                agg_ps = bank_for_scalar([P, BANK])
                 nc.tensor.matmul_mx(
                     out=agg_ps[:],
                     lhsT=g_words[:, b, channels].bitcast(FP8X4),
@@ -204,27 +224,47 @@ def tile_modulatedgraphconv_pa_e_kernel(tc, x, W_words, W_scales, M, adj, adj2, 
                     start=True,
                     stop=True,
                 )
-                nc.vector.scalar_tensor_tensor(
-                    out=out_t[:, h, :],
-                    in0=agg_ps[:],
-                    scalar=bias_col[:, h : h + 1],
-                    in1=self_t[:],
-                    op0=ALU.add,
-                    op1=ALU.add,
-                )
-            out_sb = work.tile([P, PACK, COUT], F32)
+                nc.scalar.activation(out=agg_t[b][:, h, :], in_=agg_ps[:], func=ACT.Identity, bias=bias_col[:, h : h + 1])
+
+        def finish(b):
+            out_sb = per_batch.tile([P, PACK, COUT], F32, name="out_sb")
+            out_rows = out[b].rearrange("(p t) c -> p t c", t=PACK)
             for first_slot in range(0, PACK, 2):
-                back_ps = psum.tile([P, 2, COUT], F32, tag="back")
+                back_ps = bank_for_vector([P, 2, COUT])
                 for s in range(2):
                     nodes = slice((first_slot + s) * P, (first_slot + s + 1) * P)
                     for h in range(HALVES):
-                        nc.tensor.transpose(back_ps[:, s, h * P : (h + 1) * P], out_t[:, h, nodes], ident_f32[:])
-                nc.scalar.copy(out=out_sb[:, first_slot : first_slot + 2, :], in_=back_ps[:])
-            nc.sync.dma_start(out=out[b].rearrange("(p t) c -> p t c", t=PACK), in_=out_sb[:])
+                        nc.tensor.transpose(back_ps[:, s, h * P : (h + 1) * P], agg_t[b][:, h, nodes], ident_f32[:])
+                slots = slice(first_slot, first_slot + 2)
+                nc.vector.tensor_tensor(out=out_sb[:, slots, :], in0=back_ps[:], in1=self_term[b][:, slots, :], op=ALU.add)
+                nc.sync.dma_start(out=out_rows[:, slots, :], in_=out_sb[:, slots, :])
 
-        project(0)
-        adjacency()
-        for b in range(1, BATCH):
-            project(b)
-            combine(b - 1)
-        combine(BATCH - 1)
+        transpose_x(0)
+        transpose_x(1)
+        quantise_x(0)
+        for b in range(BATCH):
+            project_h1(b)
+            if b + 2 < BATCH:
+                transpose_x(b + 2)
+            if b in (1, 2):
+                add_adjacency(2 * (b - 1))
+                add_adjacency(2 * (b - 1) + 1)
+            modulate(b, 0)
+            if b + 1 < BATCH:
+                quantise_x(b + 1)
+            modulate(b, 1)
+            if b >= 1:
+                quantise_g(b - 1)
+        quantise_g(BATCH - 1)
+        self_gain()
+        bias_onto_partitions()
+        symmetrise()
+        weigh_self(0)
+        weigh_self(1)
+        aggregate(0)
+        for b in range(BATCH):
+            if b + 1 < BATCH:
+                aggregate(b + 1)
+            finish(b)
+            if b + 2 < BATCH:
+                weigh_self(b + 2)

@@ -44,8 +44,19 @@ def tile_modulatedgraphconv_pa_e_kernel(tc, x, W_words, W_scales, M, adj, adj2, 
         adj_sb = keep.tile([P, PACK, NODES], BF16)
         adj2_sb = keep.tile([P, PACK, NODES], BF16)
 
+        diag_adj = keep.tile([P, PACK], BF16)
+        diag_adj2 = keep.tile([P, PACK], BF16)
+
         def load_x(b):
-            nc.sync.dma_start(out=x_sb[b][:], in_=x[b].rearrange("(p t) k -> p t k", t=PACK))
+            rows = x[b].rearrange("(p t) k -> p t k", t=PACK)
+            for first_slot in range(0, PACK, 2):
+                slots = slice(first_slot, first_slot + 2)
+                nc.sync.dma_start(out=x_sb[b][:, slots, :], in_=rows[:, slots, :])
+
+        def load_diagonal(dest, matrix):
+            diagonal = matrix.rearrange("i j -> (i j)")[0 : NODES * NODES : NODES + 1]
+            with nc.allow_non_contiguous_dma(reason="the diagonal of a matrix is 512 single elements"):
+                nc.sync.dma_start(out=dest[:], in_=diagonal.rearrange("(p t) -> p t", t=PACK))
 
         load_x(0)
         load_x(1)
@@ -60,6 +71,8 @@ def tile_modulatedgraphconv_pa_e_kernel(tc, x, W_words, W_scales, M, adj, adj2, 
                 in_=W_scales[:, 4 * quadrant : 4 * quadrant + 4, :].rearrange("e r n -> r e n").bitcast(I32),
             )
         nc.sync.dma_start(out=m_sb[:], in_=M.rearrange("(p t) c -> p t c", t=PACK))
+        load_diagonal(diag_adj, adj)
+        load_diagonal(diag_adj2, adj2)
         load_x(2)
         load_x(3)
         nc.sync.dma_start(out=adj_sb[:], in_=adj.rearrange("(p t) i -> p t i", t=PACK))
@@ -72,11 +85,7 @@ def tile_modulatedgraphconv_pa_e_kernel(tc, x, W_words, W_scales, M, adj, adj2, 
         ident_bf16 = keep.tile([P, P], BF16)
         nc.vector.tensor_copy(out=ident_bf16[:], in_=ident_f32[:])
         off_diagonal = keep.tile([P, P], F32)
-        nc.vector.tensor_scalar(
-            out=off_diagonal[:], in0=ident_f32[:], scalar1=-1.0, scalar2=1.0, op0=ALU.mult, op1=ALU.add
-        )
-        twice_ident = keep.tile([P, P], F32)
-        nc.scalar.mul(out=twice_ident[:], in_=ident_f32[:], mul=2.0)
+        nc.scalar.activation(out=off_diagonal[:], in_=ident_f32[:], func=ACT.Copy, bias=1.0, scale=-1.0)
 
         xq_words = keep.tile([P, BATCH, NODES], U32, align_bytes=64)
         xq_scales = keep.tile([P, BATCH, NODES], U8, align_bytes=64)
@@ -144,14 +153,12 @@ def tile_modulatedgraphconv_pa_e_kernel(tc, x, W_words, W_scales, M, adj, adj2, 
             )
 
         half_s = keep.tile([P, PACK, PACK, P], F32)
-        diag_only = keep.tile([P, PACK, P], F32)
 
         def add_adjacency(r):
             s_ps = bank_for_scalar([P, BANK])
             nc.tensor.matmul(out=s_ps[:], lhsT=ident_bf16[:], rhs=adj_sb[:, r, :], start=True, stop=False)
             nc.tensor.matmul(out=s_ps[:], lhsT=ident_bf16[:], rhs=adj2_sb[:, r, :], start=False, stop=True)
             nc.scalar.mul(out=half_s[:, r, :, :], in_=s_ps[:].rearrange("p (q c) -> p c q", c=PACK), mul=0.5)
-            nc.gpsimd.tensor_tensor(out=diag_only[:, r, :], in0=half_s[:, r, r, :], in1=twice_ident[:], op=ALU.mult)
             nc.gpsimd.tensor_tensor(out=half_s[:, r, r, :], in0=half_s[:, r, r, :], in1=off_diagonal[:], op=ALU.mult)
 
         a_self = keep.tile([P, PACK], F32)
@@ -159,10 +166,7 @@ def tile_modulatedgraphconv_pa_e_kernel(tc, x, W_words, W_scales, M, adj, adj2, 
         bias_col = keep.tile([P, HALVES], F32)
 
         def self_gain():
-            for t in range(PACK):
-                nc.scalar.activation(
-                    out=diag_only[:, t, :], in_=diag_only[:, t, :], func=ACT.Copy, accum_out=a_self[:, t : t + 1]
-                )
+            nc.gpsimd.tensor_tensor(out=a_self[:], in0=diag_adj[:], in1=diag_adj2[:], op=ALU.add)
             for t in range(PACK):
                 nc.scalar.activation(out=gain[:, t, :], in_=m_sb[:, t, :], func=ACT.Copy, scale=a_self[:, t : t + 1])
 
@@ -192,10 +196,12 @@ def tile_modulatedgraphconv_pa_e_kernel(tc, x, W_words, W_scales, M, adj, adj2, 
         self_term = {}
         agg_t = {}
 
-        def weigh_self(b):
-            self_term[b] = per_batch.tile([P, PACK, COUT], F32, name="self_term")
+        h0_banks = {}
+
+        def project_h0(b):
             for first_slot in range(0, PACK, 2):
                 h0_ps = bank_for_vector([P, 2, COUT])
+                h0_banks[(b, first_slot)] = h0_ps
                 for s in range(2):
                     nodes = slice((first_slot + s) * P, (first_slot + s + 1) * P)
                     nc.tensor.matmul_mx(
@@ -207,8 +213,14 @@ def tile_modulatedgraphconv_pa_e_kernel(tc, x, W_words, W_scales, M, adj, adj2, 
                         start=True,
                         stop=True,
                     )
+
+        def weigh_self(b):
+            self_term[b] = per_batch.tile([P, PACK, COUT], F32, name="self_term")
+            for first_slot in range(0, PACK, 2):
                 slots = slice(first_slot, first_slot + 2)
-                nc.vector.tensor_tensor(out=self_term[b][:, slots, :], in0=h0_ps[:], in1=gain[:, slots, :], op=ALU.mult)
+                nc.vector.tensor_tensor(
+                    out=self_term[b][:, slots, :], in0=h0_banks[(b, first_slot)][:], in1=gain[:, slots, :], op=ALU.mult
+                )
 
         def aggregate(b):
             agg_t[b] = per_batch.tile([P, HALVES, NODES], F32, name="agg_t")
@@ -239,14 +251,15 @@ def tile_modulatedgraphconv_pa_e_kernel(tc, x, W_words, W_scales, M, adj, adj2, 
                 nc.vector.tensor_tensor(out=out_sb[:, slots, :], in0=back_ps[:], in1=self_term[b][:, slots, :], op=ALU.add)
                 nc.sync.dma_start(out=out_rows[:, slots, :], in_=out_sb[:, slots, :])
 
-        transpose_x(0)
-        transpose_x(1)
-        quantise_x(0)
-        for b in range(BATCH):
+        def first_stage(b):
             project_h1(b)
+            if 1 <= b < BATCH - 1:
+                project_h0(b - 1)
             if b + 2 < BATCH:
                 transpose_x(b + 2)
-            if b in (1, 2):
+            if b == 0:
+                self_gain()
+            if 1 <= b < BATCH - 1:
                 add_adjacency(2 * (b - 1))
                 add_adjacency(2 * (b - 1) + 1)
             modulate(b, 0)
@@ -255,16 +268,23 @@ def tile_modulatedgraphconv_pa_e_kernel(tc, x, W_words, W_scales, M, adj, adj2, 
             modulate(b, 1)
             if b >= 1:
                 quantise_g(b - 1)
-        quantise_g(BATCH - 1)
-        self_gain()
+            if 1 <= b < BATCH - 1:
+                weigh_self(b - 1)
+
+        transpose_x(0)
+        transpose_x(1)
+        quantise_x(0)
+        for b in range(BATCH - 1):
+            first_stage(b)
         bias_onto_partitions()
         symmetrise()
-        weigh_self(0)
-        weigh_self(1)
+        first_stage(BATCH - 1)
+        quantise_g(BATCH - 1)
         aggregate(0)
+        for b in range(BATCH - 2, BATCH):
+            project_h0(b)
+            weigh_self(b)
         for b in range(BATCH):
             if b + 1 < BATCH:
                 aggregate(b + 1)
             finish(b)
-            if b + 2 < BATCH:
-                weigh_self(b + 2)

@@ -17,6 +17,10 @@ PACK = 4
 BATCH, NODES, CIN, COUT = 4, 512, 512, 256
 HALVES = COUT // P
 BANK = 512
+PAIR = BANK // COUT
+QUADRANT = 32
+SCALE_ROWS = QUADRANT // 8
+SCALAR_RING, VECTOR_RING = 3, 5
 
 FLOPS = 2 * BATCH * NODES * CIN * 2 * COUT + 2 * BATCH * NODES * NODES * COUT
 
@@ -29,10 +33,10 @@ def tile_modulatedgraphconv_pa_e_kernel(tc, x, W_words, W_scales, M, adj, adj2, 
         psum = ctx.enter_context(tc.psum_pool(name="psum", bufs=1))
 
         def bank_for_scalar(shape, dtype=F32):
-            return psum.tile(shape, dtype, name="bank_for_scalar", tag="for_scalar", bufs=3)
+            return psum.tile(shape, dtype, name="bank_for_scalar", tag="for_scalar", bufs=SCALAR_RING)
 
         def bank_for_vector(shape):
-            return psum.tile(shape, F32, name="bank_for_vector", tag="for_vector", bufs=5)
+            return psum.tile(shape, F32, name="bank_for_vector", tag="for_vector", bufs=VECTOR_RING)
 
         ctx.enter_context(tc.manual_schedule())
 
@@ -40,17 +44,16 @@ def tile_modulatedgraphconv_pa_e_kernel(tc, x, W_words, W_scales, M, adj, adj2, 
         w_words = keep.tile([P, 2 * COUT], U32, align_bytes=64)
         w_scales = keep.tile([P, 2 * COUT], U8, align_bytes=64)
         m_sb = keep.tile([P, PACK, COUT], BF16)
-        bias_rows = keep.tile([P, P], BF16)
-        adj_sb = keep.tile([P, PACK, NODES], BF16)
-        adj2_sb = keep.tile([P, PACK, NODES], BF16)
-
         diag_adj = keep.tile([P, PACK], BF16)
         diag_adj2 = keep.tile([P, PACK], BF16)
+        adj_sb = keep.tile([P, PACK, NODES], BF16)
+        adj2_sb = keep.tile([P, PACK, NODES], BF16)
+        bias_rows = keep.tile([P, P], BF16)
 
         def load_x(b):
             rows = x[b].rearrange("(p t) k -> p t k", t=PACK)
-            for first_slot in range(0, PACK, 2):
-                slots = slice(first_slot, first_slot + 2)
+            for first_slot in range(0, PACK, PAIR):
+                slots = slice(first_slot, first_slot + PAIR)
                 nc.sync.dma_start(out=x_sb[b][:, slots, :], in_=rows[:, slots, :])
 
         def load_diagonal(dest, matrix):
@@ -65,10 +68,12 @@ def tile_modulatedgraphconv_pa_e_kernel(tc, x, W_words, W_scales, M, adj, adj2, 
             in_=W_words.rearrange("e p n t -> p e (n t)").bitcast(I32),
         )
         nc.vector.memset(w_scales[:].bitcast(I32), 0)
-        for quadrant in range(4):
+        for quadrant in range(P // QUADRANT):
+            live = slice(QUADRANT * quadrant, QUADRANT * quadrant + SCALE_ROWS)
+            rows = slice(SCALE_ROWS * quadrant, SCALE_ROWS * (quadrant + 1))
             nc.sync.dma_start(
-                out=w_scales[32 * quadrant : 32 * quadrant + 4, :].bitcast(I32).rearrange("r (e n) -> r e n", e=2),
-                in_=W_scales[:, 4 * quadrant : 4 * quadrant + 4, :].rearrange("e r n -> r e n").bitcast(I32),
+                out=w_scales[live, :].bitcast(I32).rearrange("r (e n) -> r e n", e=2),
+                in_=W_scales[:, rows, :].rearrange("e r n -> r e n").bitcast(I32),
             )
         nc.sync.dma_start(out=m_sb[:], in_=M.rearrange("(p t) c -> p t c", t=PACK))
         load_diagonal(diag_adj, adj)
@@ -95,21 +100,19 @@ def tile_modulatedgraphconv_pa_e_kernel(tc, x, W_words, W_scales, M, adj, adj2, 
         a_scales = keep.tile([P, NODES], U8, align_bytes=64)
 
         x_grouped = {}
-        h1_banks = {}
-        g_grouped = {}
 
         def transpose_x(b):
             x_pairs = x_sb[b][:].rearrange("p t k -> p (t k)").bitcast(F32)
             x_pairs = x_pairs.rearrange("p (t w u) -> p t w u", t=PACK, u=2)
             x_grouped[b] = per_batch.tile([P, NODES * PACK], BF16, name="x_grouped", align_bytes=64)
             grouped_pairs = x_grouped[b][:].bitcast(F32).rearrange("p (s r u) -> p s r u", s=PACK, u=2)
-            for first_slot in range(0, PACK, 2):
-                xt_ps = bank_for_scalar([P, 2, 2, P])
-                for s in range(2):
+            for first_slot in range(0, PACK, PAIR):
+                xt_ps = bank_for_scalar([P, PAIR, 2, P])
+                for s in range(PAIR):
                     for u in range(2):
                         nc.tensor.transpose(xt_ps[:, s, u, :], x_pairs[:, first_slot + s, :, u], ident_f32[:])
                 nc.scalar.copy(
-                    out=grouped_pairs[:, first_slot : first_slot + 2, :, :],
+                    out=grouped_pairs[:, first_slot : first_slot + PAIR, :, :],
                     in_=xt_ps[:].rearrange("p s u r -> p s r u"),
                 )
 
@@ -117,6 +120,9 @@ def tile_modulatedgraphconv_pa_e_kernel(tc, x, W_words, W_scales, M, adj, adj2, 
             nc.vector.quantize_mx(
                 out=xq_words[:, b, :].bitcast(FP8X4), scales=xq_scales[:, b, :], in_=x_grouped[b][:]
             )
+
+        h1_banks = {}
+        g_grouped = {}
 
         def project_h1(b):
             for h in range(HALVES):
@@ -153,6 +159,7 @@ def tile_modulatedgraphconv_pa_e_kernel(tc, x, W_words, W_scales, M, adj, adj2, 
             )
 
         half_s = keep.tile([P, PACK, PACK, P], F32)
+        a_grouped = keep.tile([P, PACK, P, PACK], BF16, align_bytes=64)
 
         def add_adjacency(r):
             s_ps = bank_for_scalar([P, BANK])
@@ -161,22 +168,7 @@ def tile_modulatedgraphconv_pa_e_kernel(tc, x, W_words, W_scales, M, adj, adj2, 
             nc.scalar.mul(out=half_s[:, r, :, :], in_=s_ps[:].rearrange("p (q c) -> p c q", c=PACK), mul=0.5)
             nc.gpsimd.tensor_tensor(out=half_s[:, r, r, :], in0=half_s[:, r, r, :], in1=off_diagonal[:], op=ALU.mult)
 
-        a_self = keep.tile([P, PACK], F32)
-        gain = keep.tile([P, PACK, COUT], F32)
-        bias_col = keep.tile([P, HALVES], F32)
-
-        def self_gain():
-            nc.gpsimd.tensor_tensor(out=a_self[:], in0=diag_adj[:], in1=diag_adj2[:], op=ALU.add)
-            for t in range(PACK):
-                nc.scalar.activation(out=gain[:, t, :], in_=m_sb[:, t, :], func=ACT.Copy, scale=a_self[:, t : t + 1])
-
-        def bias_onto_partitions():
-            bias_ps = bank_for_scalar([P, P], BF16)
-            nc.tensor.transpose(bias_ps[:], bias_rows[:], ident_bf16[:])
-            nc.scalar.copy(out=bias_col[:], in_=bias_ps[:, 0:HALVES])
-
         def symmetrise():
-            a_grouped = keep.tile([P, PACK, P, PACK], BF16, align_bytes=64)
             for c in range(PACK):
                 st_ps = bank_for_vector([P, PACK, P])
                 for t in range(PACK):
@@ -187,25 +179,31 @@ def tile_modulatedgraphconv_pa_e_kernel(tc, x, W_words, W_scales, M, adj, adj2, 
                     in1=half_s[:, :, c, :].rearrange("p t q -> p q t"),
                     op=ALU.add,
                 )
+
+        def quantise_a():
             nc.vector.quantize_mx(
                 out=a_words[:].bitcast(FP8X4),
                 scales=a_scales[:],
                 in_=a_grouped[:].rearrange("p c q t -> p (c q t)"),
             )
 
-        self_term = {}
-        agg_t = {}
-
+        a_self = keep.tile([P, PACK], F32)
+        gain = keep.tile([P, PACK, COUT], F32)
         h0_banks = {}
+        self_term = {}
+
+        def self_gain():
+            nc.gpsimd.tensor_tensor(out=a_self[:], in0=diag_adj[:], in1=diag_adj2[:], op=ALU.add)
+            for t in range(PACK):
+                nc.scalar.activation(out=gain[:, t, :], in_=m_sb[:, t, :], func=ACT.Copy, scale=a_self[:, t : t + 1])
 
         def project_h0(b):
-            for first_slot in range(0, PACK, 2):
-                h0_ps = bank_for_vector([P, 2, COUT])
-                h0_banks[(b, first_slot)] = h0_ps
-                for s in range(2):
+            for first_slot in range(0, PACK, PAIR):
+                h0_banks[(b, first_slot)] = bank_for_vector([P, PAIR, COUT])
+                for s in range(PAIR):
                     nodes = slice((first_slot + s) * P, (first_slot + s + 1) * P)
                     nc.tensor.matmul_mx(
-                        out=h0_ps[:, s, :],
+                        out=h0_banks[(b, first_slot)][:, s, :],
                         lhsT=xq_words[:, b, nodes].bitcast(FP8X4),
                         lhsT_scale=xq_scales[:, b, nodes],
                         rhs=w_words[:, 0:COUT].bitcast(FP8X4),
@@ -216,11 +214,19 @@ def tile_modulatedgraphconv_pa_e_kernel(tc, x, W_words, W_scales, M, adj, adj2, 
 
         def weigh_self(b):
             self_term[b] = per_batch.tile([P, PACK, COUT], F32, name="self_term")
-            for first_slot in range(0, PACK, 2):
-                slots = slice(first_slot, first_slot + 2)
+            for first_slot in range(0, PACK, PAIR):
+                slots = slice(first_slot, first_slot + PAIR)
                 nc.vector.tensor_tensor(
                     out=self_term[b][:, slots, :], in0=h0_banks[(b, first_slot)][:], in1=gain[:, slots, :], op=ALU.mult
                 )
+
+        bias_col = keep.tile([P, HALVES], F32)
+        agg_t = {}
+
+        def bias_onto_partitions():
+            bias_ps = bank_for_scalar([P, P], BF16)
+            nc.tensor.transpose(bias_ps[:], bias_rows[:], ident_bf16[:])
+            nc.scalar.copy(out=bias_col[:], in_=bias_ps[:, 0:HALVES])
 
         def aggregate(b):
             agg_t[b] = per_batch.tile([P, HALVES, NODES], F32, name="agg_t")
@@ -241,49 +247,47 @@ def tile_modulatedgraphconv_pa_e_kernel(tc, x, W_words, W_scales, M, adj, adj2, 
         def finish(b):
             out_sb = per_batch.tile([P, PACK, COUT], F32, name="out_sb")
             out_rows = out[b].rearrange("(p t) c -> p t c", t=PACK)
-            for first_slot in range(0, PACK, 2):
-                back_ps = bank_for_vector([P, 2, COUT])
-                for s in range(2):
+            for first_slot in range(0, PACK, PAIR):
+                back_ps = bank_for_vector([P, PAIR, COUT])
+                for s in range(PAIR):
                     nodes = slice((first_slot + s) * P, (first_slot + s + 1) * P)
                     for h in range(HALVES):
                         nc.tensor.transpose(back_ps[:, s, h * P : (h + 1) * P], agg_t[b][:, h, nodes], ident_f32[:])
-                slots = slice(first_slot, first_slot + 2)
+                slots = slice(first_slot, first_slot + PAIR)
                 nc.vector.tensor_tensor(out=out_sb[:, slots, :], in0=back_ps[:], in1=self_term[b][:, slots, :], op=ALU.add)
                 nc.sync.dma_start(out=out_rows[:, slots, :], in_=out_sb[:, slots, :])
 
-        def first_stage(b):
+        transpose_x(0)
+        transpose_x(1)
+        quantise_x(0)
+        for b in range(BATCH):
             project_h1(b)
-            if 1 <= b < BATCH - 1:
-                project_h0(b - 1)
             if b + 2 < BATCH:
                 transpose_x(b + 2)
-            if b == 0:
+            if b + 2 == BATCH:
                 self_gain()
-            if 1 <= b < BATCH - 1:
-                add_adjacency(2 * (b - 1))
-                add_adjacency(2 * (b - 1) + 1)
+                project_h0(0)
+                for r in range(PACK):
+                    add_adjacency(r)
             modulate(b, 0)
             if b + 1 < BATCH:
                 quantise_x(b + 1)
             modulate(b, 1)
             if b >= 1:
                 quantise_g(b - 1)
-            if 1 <= b < BATCH - 1:
-                weigh_self(b - 1)
-
-        transpose_x(0)
-        transpose_x(1)
-        quantise_x(0)
-        for b in range(BATCH - 1):
-            first_stage(b)
+            if b + 2 == BATCH:
+                weigh_self(0)
         bias_onto_partitions()
         symmetrise()
-        first_stage(BATCH - 1)
         quantise_g(BATCH - 1)
+        quantise_a()
+        project_h0(1)
+        project_h0(2)
         aggregate(0)
-        for b in range(BATCH - 2, BATCH):
-            project_h0(b)
+        for b in range(1, BATCH):
             weigh_self(b)
+            if b + 2 < BATCH:
+                project_h0(b + 2)
         for b in range(BATCH):
             if b + 1 < BATCH:
                 aggregate(b + 1)

@@ -20,7 +20,7 @@ BANK = 512
 PAIR = BANK // COUT
 QUADRANT = 32
 SCALE_ROWS = QUADRANT // 8
-SCALAR_RING, VECTOR_RING = 3, 5
+SCALAR_RING, VECTOR_RING = 3, 4
 
 FLOPS = 2 * BATCH * NODES * CIN * 2 * COUT + 2 * BATCH * NODES * NODES * COUT
 
@@ -39,6 +39,9 @@ def tile_modulatedgraphconv_pa_e_kernel(tc, x, W_words, W_scales, M, adj, adj2, 
             return psum.tile(shape, F32, name="bank_for_vector", tag="for_vector", bufs=VECTOR_RING)
 
         ctx.enter_context(tc.manual_schedule())
+
+        warm = keep.tile([P, P], F32)
+        nc.vector.memset(warm[:], 0.0)
 
         x_sb = [keep.tile([P, PACK, CIN], BF16, name="x_sb%d" % b) for b in range(BATCH)]
         w_words = keep.tile([P, 2 * COUT], U32, align_bytes=64)
@@ -257,11 +260,34 @@ def tile_modulatedgraphconv_pa_e_kernel(tc, x, W_words, W_scales, M, adj, adj2, 
                 nc.vector.tensor_tensor(out=out_sb[:, slots, :], in0=back_ps[:], in1=self_term[b][:, slots, :], op=ALU.add)
                 nc.sync.dma_start(out=out_rows[:, slots, :], in_=out_sb[:, slots, :])
 
+        warm_ps = psum.tile([P, BANK], F32, name="warm_ps", tag="warm", bufs=1)
+
+        def warm_up(passes):
+            for i in range(passes):
+                nc.tensor.matmul(out=warm_ps[:, 0:P], lhsT=warm[:], rhs=warm[:], start=True, stop=True)
+
+        def keep_warm(passes):
+            for i in range(passes):
+                nc.tensor.matmul_mx(
+                    out=warm_ps[:],
+                    lhsT=w_words[:, 0:P].bitcast(FP8X4),
+                    lhsT_scale=w_scales[:, 0:P],
+                    rhs=w_words[:].bitcast(FP8X4),
+                    rhs_scale=w_scales[:],
+                    start=True,
+                    stop=True,
+                )
+
+        warm_up(4)
         transpose_x(0)
+        warm_up(1)
         transpose_x(1)
+        warm_up(1)
         quantise_x(0)
+        keep_warm(1)
         for b in range(BATCH):
             project_h1(b)
+            keep_warm(0)
             if b + 2 < BATCH:
                 transpose_x(b + 2)
             if b + 2 == BATCH:

@@ -20,7 +20,7 @@ BANK = 512
 PAIR = BANK // COUT
 QUADRANT = 32
 SCALE_ROWS = QUADRANT // 8
-SCALAR_RING, VECTOR_RING = 3, 4
+SCALAR_RING, VECTOR_RING = 3, 5
 
 FLOPS = 2 * BATCH * NODES * CIN * 2 * COUT + 2 * BATCH * NODES * NODES * COUT
 
@@ -51,21 +51,20 @@ def tile_modulatedgraphconv_pa_e_kernel(tc, x, W_words, W_scales, M, adj, adj2, 
         diag_adj2 = keep.tile([P, PACK], BF16)
         adj_sb = keep.tile([P, PACK, NODES], BF16)
         adj2_sb = keep.tile([P, PACK, NODES], BF16)
-        bias_rows = keep.tile([P, P], BF16)
+        bias_rows = keep.tile([P, COUT], BF16)
 
-        def load_x(b):
-            rows = x[b].rearrange("(p t) k -> p t k", t=PACK)
-            for first_slot in range(0, PACK, PAIR):
-                slots = slice(first_slot, first_slot + PAIR)
+        def load_x(b, piece):
+            rows = x[b].rearrange("(t p) k -> p t k", t=PACK)
+            for first_slot in range(0, PACK, piece):
+                slots = slice(first_slot, first_slot + piece)
                 nc.sync.dma_start(out=x_sb[b][:, slots, :], in_=rows[:, slots, :])
 
         def load_diagonal(dest, matrix):
             diagonal = matrix.rearrange("i j -> (i j)")[0 : NODES * NODES : NODES + 1]
             with nc.allow_non_contiguous_dma(reason="the diagonal of a matrix is 512 single elements"):
-                nc.sync.dma_start(out=dest[:], in_=diagonal.rearrange("(p t) -> p t", t=PACK))
+                nc.sync.dma_start(out=dest[:], in_=diagonal.rearrange("(t p) -> p t", t=PACK))
 
-        load_x(0)
-        load_x(1)
+        load_x(0, PAIR)
         nc.sync.dma_start(
             out=w_words[:].bitcast(I32).rearrange("p (e n) -> p e n", e=2),
             in_=W_words.rearrange("e p n t -> p e (n t)").bitcast(I32),
@@ -78,22 +77,27 @@ def tile_modulatedgraphconv_pa_e_kernel(tc, x, W_words, W_scales, M, adj, adj2, 
                 out=w_scales[live, :].bitcast(I32).rearrange("r (e n) -> r e n", e=2),
                 in_=W_scales[:, rows, :].rearrange("e r n -> r e n").bitcast(I32),
             )
-        nc.sync.dma_start(out=m_sb[:], in_=M.rearrange("(p t) c -> p t c", t=PACK))
+        for first_slot in range(0, PACK, PAIR):
+            slots = slice(first_slot, first_slot + PAIR)
+            for tile, matrix in ((adj_sb, adj), (adj2_sb, adj2)):
+                nc.sync.dma_start(out=tile[:, slots, :], in_=matrix.rearrange("(t p) i -> p t i", t=PACK)[:, slots, :])
+        load_x(1, PACK)
         load_diagonal(diag_adj, adj)
         load_diagonal(diag_adj2, adj2)
-        load_x(2)
-        load_x(3)
-        nc.sync.dma_start(out=adj_sb[:], in_=adj.rearrange("(p t) i -> p t i", t=PACK))
-        nc.sync.dma_start(out=adj2_sb[:], in_=adj2.rearrange("(p t) i -> p t i", t=PACK))
-        nc.vector.memset(bias_rows[:], 0.0)
-        nc.sync.dma_start(out=bias_rows[0:HALVES, :], in_=bias.rearrange("(h c) -> h c", h=HALVES))
-
+        load_x(2, PACK)
+        load_x(3, PACK)
         ident_f32 = keep.tile([P, P], F32)
         make_identity(nc, ident_f32[:])
         ident_bf16 = keep.tile([P, P], BF16)
         nc.vector.tensor_copy(out=ident_bf16[:], in_=ident_f32[:])
-        off_diagonal = keep.tile([P, P], F32)
-        nc.scalar.activation(out=off_diagonal[:], in_=ident_f32[:], func=ACT.Copy, bias=1.0, scale=-1.0)
+        ones = keep.tile([P, P], BF16)
+        nc.vector.memset(ones[:], 1.0)
+        flip_diagonal = keep.tile([P, P], F32)
+        nc.scalar.activation(out=flip_diagonal[:], in_=ident_f32[:], func=ACT.Copy, bias=1.0, scale=-2.0)
+
+        nc.gpsimd.dma_start(out=m_sb[:], in_=M.rearrange("(t p) c -> p t c", t=PACK))
+        nc.gpsimd.memset(bias_rows[:], 0.0)
+        nc.gpsimd.dma_start(out=bias_rows[0:1, :], in_=bias.rearrange("(o c) -> o c", o=1))
 
         xq_words = keep.tile([P, BATCH, NODES], U32, align_bytes=64)
         xq_scales = keep.tile([P, BATCH, NODES], U8, align_bytes=64)
@@ -104,24 +108,27 @@ def tile_modulatedgraphconv_pa_e_kernel(tc, x, W_words, W_scales, M, adj, adj2, 
 
         x_grouped = {}
 
-        def transpose_x(b):
+        def transpose_x(b, first_slot, slots, copy):
+            if first_slot == 0:
+                x_grouped[b] = per_batch.tile([P, NODES * PACK], BF16, name="x_grouped", align_bytes=64)
             x_pairs = x_sb[b][:].rearrange("p t k -> p (t k)").bitcast(F32)
             x_pairs = x_pairs.rearrange("p (t w u) -> p t w u", t=PACK, u=2)
-            x_grouped[b] = per_batch.tile([P, NODES * PACK], BF16, name="x_grouped", align_bytes=64)
             grouped_pairs = x_grouped[b][:].bitcast(F32).rearrange("p (s r u) -> p s r u", s=PACK, u=2)
-            for first_slot in range(0, PACK, PAIR):
-                xt_ps = bank_for_scalar([P, PAIR, 2, P])
-                for s in range(PAIR):
-                    for u in range(2):
-                        nc.tensor.transpose(xt_ps[:, s, u, :], x_pairs[:, first_slot + s, :, u], ident_f32[:])
-                nc.scalar.copy(
-                    out=grouped_pairs[:, first_slot : first_slot + PAIR, :, :],
-                    in_=xt_ps[:].rearrange("p s u r -> p s r u"),
-                )
+            xt_ps = bank_for_scalar([P, slots, 2, P])
+            for s in range(slots):
+                for u in range(2):
+                    nc.tensor.transpose(xt_ps[:, s, u, :], x_pairs[:, first_slot + s, :, u], ident_f32[:])
+            copy(
+                out=grouped_pairs[:, first_slot : first_slot + slots, :, :],
+                in_=xt_ps[:].rearrange("p s u r -> p s r u"),
+            )
 
-        def quantise_x(b):
+        def quantise_x(b, first_slot=0, slots=PACK):
+            nodes = slice(first_slot * P, (first_slot + slots) * P)
             nc.vector.quantize_mx(
-                out=xq_words[:, b, :].bitcast(FP8X4), scales=xq_scales[:, b, :], in_=x_grouped[b][:]
+                out=xq_words[:, b, nodes].bitcast(FP8X4),
+                scales=xq_scales[:, b, nodes],
+                in_=x_grouped[b][:, first_slot * P * PACK : (first_slot + slots) * P * PACK],
             )
 
         h1_banks = {}
@@ -161,33 +168,38 @@ def tile_modulatedgraphconv_pa_e_kernel(tc, x, W_words, W_scales, M, adj, adj2, 
                 in_=g_grouped[b][:].rearrange("p c t -> p (c t)"),
             )
 
-        half_s = keep.tile([P, PACK, PACK, P], F32)
-        a_grouped = keep.tile([P, PACK, P, PACK], BF16, align_bytes=64)
+        sums = keep.tile([P, PACK, NODES], F32)
+        a_grouped = keep.tile([P, NODES, PACK], BF16, align_bytes=64)
+        a_banks = {}
 
-        def add_adjacency(r):
-            s_ps = bank_for_scalar([P, BANK])
-            nc.tensor.matmul(out=s_ps[:], lhsT=ident_bf16[:], rhs=adj_sb[:, r, :], start=True, stop=False)
-            nc.tensor.matmul(out=s_ps[:], lhsT=ident_bf16[:], rhs=adj2_sb[:, r, :], start=False, stop=True)
-            nc.scalar.mul(out=half_s[:, r, :, :], in_=s_ps[:].rearrange("p (q c) -> p c q", c=PACK), mul=0.5)
-            nc.gpsimd.tensor_tensor(out=half_s[:, r, r, :], in0=half_s[:, r, r, :], in1=off_diagonal[:], op=ALU.mult)
+        def add_adjacency(r, engine):
+            engine.tensor_tensor(out=sums[:, r, :], in0=adj_sb[:, r, :], in1=adj2_sb[:, r, :], op=ALU.add)
 
-        def symmetrise():
-            for c in range(PACK):
-                st_ps = bank_for_vector([P, PACK, P])
-                for t in range(PACK):
-                    nc.tensor.transpose(st_ps[:, t, :], half_s[:, c, t, :], ident_f32[:])
-                nc.vector.tensor_tensor(
-                    out=a_grouped[:, c, :, :],
-                    in0=st_ps[:].rearrange("p t q -> p q t"),
-                    in1=half_s[:, :, c, :].rearrange("p t q -> p q t"),
-                    op=ALU.add,
-                )
+        def flip_the_diagonal(r):
+            block = sums[:, r, r * P : (r + 1) * P]
+            nc.gpsimd.tensor_tensor(out=block, in0=block, in1=flip_diagonal[:], op=ALU.mult)
+
+        def transpose_adjacency(c):
+            a_banks[c] = bank_for_vector([P, PACK, P])
+            for t in range(PACK):
+                columns = slice(t * P, (t + 1) * P)
+                nc.tensor.matmul(out=a_banks[c][:, t, :], lhsT=adj_sb[:, c, columns], rhs=ident_bf16[:], start=True, stop=False)
+                nc.tensor.matmul(out=a_banks[c][:, t, :], lhsT=adj2_sb[:, c, columns], rhs=ident_bf16[:], start=False, stop=True)
+
+        def symmetrise(c):
+            columns = slice(c * P, (c + 1) * P)
+            nc.vector.tensor_tensor(
+                out=a_grouped[:, columns, :],
+                in0=a_banks[c][:].rearrange("p t q -> p q t"),
+                in1=sums[:, :, columns].rearrange("p t q -> p q t"),
+                op=ALU.add,
+            )
 
         def quantise_a():
             nc.vector.quantize_mx(
                 out=a_words[:].bitcast(FP8X4),
                 scales=a_scales[:],
-                in_=a_grouped[:].rearrange("p c q t -> p (c q t)"),
+                in_=a_grouped[:].rearrange("p i t -> p (i t)"),
             )
 
         a_self = keep.tile([P, PACK], F32)
@@ -195,43 +207,90 @@ def tile_modulatedgraphconv_pa_e_kernel(tc, x, W_words, W_scales, M, adj, adj2, 
         h0_banks = {}
         self_term = {}
 
-        def self_gain():
+        def self_diagonal():
             nc.gpsimd.tensor_tensor(out=a_self[:], in0=diag_adj[:], in1=diag_adj2[:], op=ALU.add)
-            for t in range(PACK):
-                nc.scalar.activation(out=gain[:, t, :], in_=m_sb[:, t, :], func=ACT.Copy, scale=a_self[:, t : t + 1])
 
-        def project_h0(b):
+        def self_gain(first, last):
+            for t in range(first, last):
+                nc.gpsimd.tensor_scalar(
+                    out=gain[:, t, :], in0=m_sb[:, t, :], scalar1=a_self[:, t : t + 1], scalar2=0.0, op0=ALU.mult, op1=ALU.add
+                )
+
+        def new_self_term(b):
+            self_term[b] = per_batch.tile([P, PACK, COUT], F32, name="self_term")
+
+        def project_h0(b, first_slot, bank):
+            for s in range(PAIR):
+                nodes = slice((first_slot + s) * P, (first_slot + s + 1) * P)
+                nc.tensor.matmul_mx(
+                    out=bank[:, s, :],
+                    lhsT=xq_words[:, b, nodes].bitcast(FP8X4),
+                    lhsT_scale=xq_scales[:, b, nodes],
+                    rhs=w_words[:, 0:COUT].bitcast(FP8X4),
+                    rhs_scale=w_scales[:, 0:COUT],
+                    start=True,
+                    stop=True,
+                )
+
+        def h0_on_vector(b, first_slot):
+            h0_banks[(b, first_slot)] = bank_for_vector([P, PAIR, COUT])
+            project_h0(b, first_slot, h0_banks[(b, first_slot)])
+
+        def weigh_on_vector(b, first_slot):
+            slots = slice(first_slot, first_slot + PAIR)
+            nc.vector.tensor_tensor(
+                out=self_term[b][:, slots, :], in0=h0_banks[(b, first_slot)][:], in1=gain[:, slots, :], op=ALU.mult
+            )
+
+        def bring_h0(b, first_slot):
+            bank = bank_for_scalar([P, PAIR, COUT])
+            project_h0(b, first_slot, bank)
+            slots = slice(first_slot, first_slot + PAIR)
+            nc.scalar.copy(out=self_term[b][:, slots, :], in_=bank[:])
+
+        def weigh(b, first_slot):
+            term = self_term[b][:, first_slot : first_slot + PAIR, :]
+            nc.gpsimd.tensor_tensor(out=term, in0=term, in1=gain[:, first_slot : first_slot + PAIR, :], op=ALU.mult)
+
+        bias_pair = keep.tile([P, PAIR, COUT], F32)
+        bias_col = keep.tile([P, HALVES], F32)
+        agg_t = {}
+        agg_banks = {}
+
+        def bias_onto_partitions():
+            for h in range(HALVES):
+                col_ps = bank_for_scalar([P, P], BF16)
+                nc.tensor.transpose(col_ps[:], bias_rows[:, h * P : (h + 1) * P], ident_bf16[:])
+                nc.scalar.copy(out=bias_col[:, h : h + 1], in_=col_ps[:, 0:1])
+
+        def spread_bias():
+            bias_ps = bank_for_scalar([P, HALVES, P])
+            for h in range(HALVES):
+                nc.tensor.transpose(bias_ps[:, h, :], bias_col[:, h : h + 1].to_broadcast([P, P]), ident_f32[:])
+            for s in range(PAIR):
+                nc.scalar.copy(out=bias_pair[:, s, :], in_=bias_ps[:].rearrange("p h c -> p (h c)"))
+
+        def add_bias(b, first_slot):
+            slots = slice(first_slot, first_slot + PAIR)
+            nc.gpsimd.tensor_tensor(out=self_term[b][:, slots, :], in0=self_term[b][:, slots, :], in1=bias_pair[:], op=ALU.add)
+
+        def aggregate(b):
             for first_slot in range(0, PACK, PAIR):
-                h0_banks[(b, first_slot)] = bank_for_vector([P, PAIR, COUT])
+                bank = bank_for_vector([P, PAIR, COUT])
+                agg_banks[(b, first_slot)] = bank
                 for s in range(PAIR):
                     nodes = slice((first_slot + s) * P, (first_slot + s + 1) * P)
                     nc.tensor.matmul_mx(
-                        out=h0_banks[(b, first_slot)][:, s, :],
-                        lhsT=xq_words[:, b, nodes].bitcast(FP8X4),
-                        lhsT_scale=xq_scales[:, b, nodes],
-                        rhs=w_words[:, 0:COUT].bitcast(FP8X4),
-                        rhs_scale=w_scales[:, 0:COUT],
+                        out=bank[:, s, :],
+                        lhsT=a_words[:, nodes].bitcast(FP8X4),
+                        lhsT_scale=a_scales[:, nodes],
+                        rhs=g_words[:, b, :].bitcast(FP8X4),
+                        rhs_scale=g_scales[:, b, :],
                         start=True,
                         stop=True,
                     )
 
-        def weigh_self(b):
-            self_term[b] = per_batch.tile([P, PACK, COUT], F32, name="self_term")
-            for first_slot in range(0, PACK, PAIR):
-                slots = slice(first_slot, first_slot + PAIR)
-                nc.vector.tensor_tensor(
-                    out=self_term[b][:, slots, :], in0=h0_banks[(b, first_slot)][:], in1=gain[:, slots, :], op=ALU.mult
-                )
-
-        bias_col = keep.tile([P, HALVES], F32)
-        agg_t = {}
-
-        def bias_onto_partitions():
-            bias_ps = bank_for_scalar([P, P], BF16)
-            nc.tensor.transpose(bias_ps[:], bias_rows[:], ident_bf16[:])
-            nc.scalar.copy(out=bias_col[:], in_=bias_ps[:, 0:HALVES])
-
-        def aggregate(b):
+        def aggregate_transposed(b):
             agg_t[b] = per_batch.tile([P, HALVES, NODES], F32, name="agg_t")
             for h in range(HALVES):
                 channels = slice(h * P, (h + 1) * P)
@@ -245,28 +304,37 @@ def tile_modulatedgraphconv_pa_e_kernel(tc, x, W_words, W_scales, M, adj, adj2, 
                     start=True,
                     stop=True,
                 )
-                nc.scalar.activation(out=agg_t[b][:, h, :], in_=agg_ps[:], func=ACT.Identity, bias=bias_col[:, h : h + 1])
+                nc.scalar.activation(
+                    out=agg_t[b][:, h, :], in_=agg_ps[:], func=ACT.Identity, bias=bias_col[:, h : h + 1], scale=0.5
+                )
 
-        def finish(b):
-            out_sb = per_batch.tile([P, PACK, COUT], F32, name="out_sb")
-            out_rows = out[b].rearrange("(p t) c -> p t c", t=PACK)
+        def transpose_back(b):
             for first_slot in range(0, PACK, PAIR):
-                back_ps = bank_for_vector([P, PAIR, COUT])
+                bank = bank_for_vector([P, PAIR, COUT])
+                agg_banks[(b, first_slot)] = bank
                 for s in range(PAIR):
                     nodes = slice((first_slot + s) * P, (first_slot + s + 1) * P)
                     for h in range(HALVES):
-                        nc.tensor.transpose(back_ps[:, s, h * P : (h + 1) * P], agg_t[b][:, h, nodes], ident_f32[:])
-                slots = slice(first_slot, first_slot + PAIR)
-                nc.vector.tensor_tensor(out=out_sb[:, slots, :], in0=back_ps[:], in1=self_term[b][:, slots, :], op=ALU.add)
-                nc.sync.dma_start(out=out_rows[:, slots, :], in_=out_sb[:, slots, :])
+                        nc.tensor.transpose(bank[:, s, h * P : (h + 1) * P], agg_t[b][:, h, nodes], ident_f32[:])
 
-        warm_ps = psum.tile([P, BANK], F32, name="warm_ps", tag="warm", bufs=1)
+        out_sb = {}
+
+        def finish(b, first_slot):
+            if first_slot == 0:
+                out_sb[b] = per_batch.tile([P, PACK, COUT], F32, name="out_sb")
+            slots = slice(first_slot, first_slot + PAIR)
+            nc.vector.tensor_tensor(
+                out=out_sb[b][:, slots, :], in0=agg_banks[(b, first_slot)][:], in1=self_term[b][:, slots, :], op=ALU.add
+            )
+            nc.sync.dma_start(out=out[b].rearrange("(t p) c -> p t c", t=PACK)[:, slots, :], in_=out_sb[b][:, slots, :])
 
         def warm_up(passes):
+            warm_ps = bank_for_vector([P, P])
             for i in range(passes):
-                nc.tensor.matmul(out=warm_ps[:, 0:P], lhsT=warm[:], rhs=warm[:], start=True, stop=True)
+                nc.tensor.matmul(out=warm_ps[:], lhsT=warm[:], rhs=warm[:], start=True, stop=True)
 
         def keep_warm(passes):
+            warm_ps = bank_for_vector([P, BANK])
             for i in range(passes):
                 nc.tensor.matmul_mx(
                     out=warm_ps[:],
@@ -278,43 +346,86 @@ def tile_modulatedgraphconv_pa_e_kernel(tc, x, W_words, W_scales, M, adj, adj2, 
                     stop=True,
                 )
 
+        for b in range(BATCH):
+            new_self_term(b)
         warm_up(4)
-        transpose_x(0)
-        warm_up(1)
-        transpose_x(1)
-        warm_up(1)
-        quantise_x(0)
-        keep_warm(1)
-        for b in range(BATCH):
-            project_h1(b)
-            keep_warm(0)
-            if b + 2 < BATCH:
-                transpose_x(b + 2)
-            if b + 2 == BATCH:
-                self_gain()
-                project_h0(0)
-                for r in range(PACK):
-                    add_adjacency(r)
-            modulate(b, 0)
-            if b + 1 < BATCH:
-                quantise_x(b + 1)
-            modulate(b, 1)
-            if b >= 1:
-                quantise_g(b - 1)
-            if b + 2 == BATCH:
-                weigh_self(0)
+        transpose_x(0, 0, PAIR, nc.scalar.copy)
+        warm_up(2)
+        transpose_x(0, PAIR, PAIR, nc.vector.tensor_copy)
+        quantise_x(0, 0, PAIR)
+        add_adjacency(0, nc.gpsimd)
+        add_adjacency(1, nc.vector)
+        quantise_x(0, PAIR, PAIR)
+        add_adjacency(2, nc.gpsimd)
+        add_adjacency(3, nc.vector)
+        for r in range(PACK):
+            flip_the_diagonal(r)
+        self_diagonal()
+        self_gain(0, PACK)
+        transpose_adjacency(0)
+        transpose_adjacency(1)
+        bring_h0(0, 0)
+        project_h1(0)
+        modulate(0, 0)
+        modulate(0, 1)
+        transpose_adjacency(2)
+        transpose_x(1, 0, PAIR, nc.scalar.copy)
+        transpose_x(1, PAIR, PAIR, nc.scalar.copy)
+        symmetrise(0)
+        symmetrise(1)
+        quantise_g(0)
+        transpose_adjacency(3)
+        quantise_x(1)
+        symmetrise(2)
+        weigh(0, 0)
+        transpose_x(2, 0, PAIR, nc.scalar.copy)
+        transpose_x(2, PAIR, PAIR, nc.scalar.copy)
+        symmetrise(3)
+        bring_h0(0, PAIR)
+        project_h1(1)
         bias_onto_partitions()
-        symmetrise()
-        quantise_g(BATCH - 1)
+        transpose_x(3, 0, PAIR, nc.scalar.copy)
+        transpose_x(3, PAIR, PAIR, nc.scalar.copy)
+        modulate(1, 0)
         quantise_a()
-        project_h0(1)
-        project_h0(2)
-        aggregate(0)
-        for b in range(1, BATCH):
-            weigh_self(b)
-            if b + 2 < BATCH:
-                project_h0(b + 2)
-        for b in range(BATCH):
-            if b + 1 < BATCH:
-                aggregate(b + 1)
-            finish(b)
+        quantise_x(2)
+        modulate(1, 1)
+        weigh(0, PAIR)
+        bring_h0(1, 0)
+        aggregate_transposed(0)
+        project_h1(2)
+        quantise_x(3)
+        modulate(2, 0)
+        quantise_g(1)
+        modulate(2, 1)
+        bring_h0(1, PAIR)
+        project_h1(3)
+        weigh(1, 0)
+        weigh(1, PAIR)
+        modulate(3, 0)
+        quantise_g(2)
+        aggregate_transposed(1)
+        transpose_back(0)
+        modulate(3, 1)
+        bring_h0(2, 0)
+        bring_h0(2, PAIR)
+        weigh(2, 0)
+        weigh(2, PAIR)
+        aggregate_transposed(2)
+        finish(0, 0)
+        quantise_g(3)
+        finish(0, PAIR)
+        transpose_back(1)
+        bring_h0(3, 0)
+        bring_h0(3, PAIR)
+        weigh(3, 0)
+        weigh(3, PAIR)
+        finish(1, 0)
+        finish(1, PAIR)
+        aggregate_transposed(3)
+        transpose_back(2)
+        finish(2, 0)
+        finish(2, PAIR)
+        transpose_back(3)
+        finish(3, 0)
+        finish(3, PAIR)

@@ -92,8 +92,9 @@ def tile_modulatedgraphconv_pa_e_kernel(tc, x, W_words, W_scales, M, adj, adj2, 
         nc.vector.tensor_copy(out=ident_bf16[:], in_=ident_f32[:])
         ones = keep.tile([P, P], BF16)
         nc.vector.memset(ones[:], 1.0)
-        flip_diagonal = keep.tile([P, P], F32)
-        nc.scalar.activation(out=flip_diagonal[:], in_=ident_f32[:], func=ACT.Copy, bias=1.0, scale=-2.0)
+        flip_diagonal = keep.tile([P, PACK, P], F32)
+        for r in range(PACK):
+            nc.scalar.activation(out=flip_diagonal[:, r, :], in_=ident_f32[:], func=ACT.Copy, bias=1.0, scale=-2.0)
 
         nc.gpsimd.dma_start(out=m_sb[:], in_=M.rearrange("(t p) c -> p t c", t=PACK))
         nc.gpsimd.memset(bias_rows[:], 0.0)
@@ -168,16 +169,17 @@ def tile_modulatedgraphconv_pa_e_kernel(tc, x, W_words, W_scales, M, adj, adj2, 
                 in_=g_grouped[b][:].rearrange("p c t -> p (c t)"),
             )
 
-        sums = keep.tile([P, PACK, NODES], F32)
+        sums_run = keep.tile([P, PACK * (NODES + P)], F32)
+        sums = sums_run[:, 0 : PACK * NODES].rearrange("p (r i) -> p r i", r=PACK)
+        squares = sums_run[:].rearrange("p (r w) -> p r w", r=PACK)[:, :, 0:P]
         a_grouped = keep.tile([P, NODES, PACK], BF16, align_bytes=64)
         a_banks = {}
 
         def add_adjacency(r, engine):
             engine.tensor_tensor(out=sums[:, r, :], in0=adj_sb[:, r, :], in1=adj2_sb[:, r, :], op=ALU.add)
 
-        def flip_the_diagonal(r):
-            block = sums[:, r, r * P : (r + 1) * P]
-            nc.gpsimd.tensor_tensor(out=block, in0=block, in1=flip_diagonal[:], op=ALU.mult)
+        def flip_the_diagonal():
+            nc.gpsimd.tensor_tensor(out=squares, in0=squares, in1=flip_diagonal[:], op=ALU.mult)
 
         def transpose_adjacency(c):
             a_banks[c] = bank_for_vector([P, PACK, P])
@@ -212,9 +214,7 @@ def tile_modulatedgraphconv_pa_e_kernel(tc, x, W_words, W_scales, M, adj, adj2, 
 
         def self_gain(first, last):
             for t in range(first, last):
-                nc.gpsimd.tensor_scalar(
-                    out=gain[:, t, :], in0=m_sb[:, t, :], scalar1=a_self[:, t : t + 1], scalar2=0.0, op0=ALU.mult, op1=ALU.add
-                )
+                nc.scalar.activation(out=gain[:, t, :], in_=m_sb[:, t, :], func=ACT.Copy, scale=a_self[:, t : t + 1])
 
         def new_self_term(b):
             self_term[b] = per_batch.tile([P, PACK, COUT], F32, name="self_term")
@@ -249,8 +249,9 @@ def tile_modulatedgraphconv_pa_e_kernel(tc, x, W_words, W_scales, M, adj, adj2, 
             nc.scalar.copy(out=self_term[b][:, slots, :], in_=bank[:])
 
         def weigh(b, first_slot):
-            term = self_term[b][:, first_slot : first_slot + PAIR, :]
-            nc.gpsimd.tensor_tensor(out=term, in0=term, in1=gain[:, first_slot : first_slot + PAIR, :], op=ALU.mult)
+            for t in range(first_slot, first_slot + PAIR):
+                term = self_term[b][:, t, :]
+                nc.gpsimd.tensor_tensor(out=term, in0=term, in1=gain[:, t, :], op=ALU.mult)
 
         bias_pair = keep.tile([P, PAIR, COUT], F32)
         bias_col = keep.tile([P, HALVES], F32)
@@ -350,40 +351,38 @@ def tile_modulatedgraphconv_pa_e_kernel(tc, x, W_words, W_scales, M, adj, adj2, 
             new_self_term(b)
         warm_up(4)
         transpose_x(0, 0, PAIR, nc.scalar.copy)
-        warm_up(2)
         transpose_x(0, PAIR, PAIR, nc.vector.tensor_copy)
+        warm_up(2)
         quantise_x(0, 0, PAIR)
-        add_adjacency(0, nc.gpsimd)
-        add_adjacency(1, nc.vector)
         quantise_x(0, PAIR, PAIR)
-        add_adjacency(2, nc.gpsimd)
-        add_adjacency(3, nc.vector)
         for r in range(PACK):
-            flip_the_diagonal(r)
+            add_adjacency(r, nc.vector)
+        flip_the_diagonal()
         self_diagonal()
-        self_gain(0, PACK)
         transpose_adjacency(0)
         transpose_adjacency(1)
         bring_h0(0, 0)
         project_h1(0)
         modulate(0, 0)
         modulate(0, 1)
+        bring_h0(0, PAIR)
         transpose_adjacency(2)
+        bias_onto_partitions()
         transpose_x(1, 0, PAIR, nc.scalar.copy)
         transpose_x(1, PAIR, PAIR, nc.scalar.copy)
         symmetrise(0)
         symmetrise(1)
         quantise_g(0)
+        self_gain(0, PACK)
+        weigh(0, 0)
         transpose_adjacency(3)
         quantise_x(1)
         symmetrise(2)
-        weigh(0, 0)
         transpose_x(2, 0, PAIR, nc.scalar.copy)
         transpose_x(2, PAIR, PAIR, nc.scalar.copy)
         symmetrise(3)
-        bring_h0(0, PAIR)
         project_h1(1)
-        bias_onto_partitions()
+        bring_h0(1, 0)
         transpose_x(3, 0, PAIR, nc.scalar.copy)
         transpose_x(3, PAIR, PAIR, nc.scalar.copy)
         modulate(1, 0)
@@ -391,35 +390,34 @@ def tile_modulatedgraphconv_pa_e_kernel(tc, x, W_words, W_scales, M, adj, adj2, 
         quantise_x(2)
         modulate(1, 1)
         weigh(0, PAIR)
-        bring_h0(1, 0)
+        weigh(1, 0)
+        bring_h0(1, PAIR)
+        weigh(1, PAIR)
         aggregate_transposed(0)
         project_h1(2)
         quantise_x(3)
         modulate(2, 0)
         quantise_g(1)
         modulate(2, 1)
-        bring_h0(1, PAIR)
-        project_h1(3)
-        weigh(1, 0)
-        weigh(1, PAIR)
-        modulate(3, 0)
-        quantise_g(2)
-        aggregate_transposed(1)
-        transpose_back(0)
-        modulate(3, 1)
         bring_h0(2, 0)
         bring_h0(2, PAIR)
         weigh(2, 0)
         weigh(2, PAIR)
-        aggregate_transposed(2)
-        finish(0, 0)
-        quantise_g(3)
-        finish(0, PAIR)
-        transpose_back(1)
+        project_h1(3)
+        aggregate_transposed(1)
+        modulate(3, 0)
+        quantise_g(2)
+        transpose_back(0)
+        modulate(3, 1)
         bring_h0(3, 0)
-        bring_h0(3, PAIR)
         weigh(3, 0)
-        weigh(3, PAIR)
+        aggregate_transposed(2)
+        quantise_g(3)
+        finish(0, 0)
+        finish(0, PAIR)
+        h0_on_vector(3, PAIR)
+        weigh_on_vector(3, PAIR)
+        transpose_back(1)
         finish(1, 0)
         finish(1, PAIR)
         aggregate_transposed(3)

@@ -360,27 +360,28 @@ def tile_modulatedgraphconv_pa_e_kernel(tc, x, W_words, W_scales, M, adj, adj2, 
         flip_the_diagonal()
         self_diagonal()
         transpose_adjacency(0)
-        transpose_adjacency(1)
         bring_h0(0, 0)
+        bring_h0(0, PAIR)
         project_h1(0)
+        transpose_adjacency(1)
         modulate(0, 0)
         modulate(0, 1)
-        bring_h0(0, PAIR)
-        transpose_adjacency(2)
-        bias_onto_partitions()
         transpose_x(1, 0, PAIR, nc.scalar.copy)
         transpose_x(1, PAIR, PAIR, nc.scalar.copy)
+        quantise_g(0)
         symmetrise(0)
         symmetrise(1)
-        quantise_g(0)
-        self_gain(0, PACK)
-        weigh(0, 0)
-        transpose_adjacency(3)
+        transpose_adjacency(2)
         quantise_x(1)
-        symmetrise(2)
+        self_gain(0, PAIR)
+        weigh(0, 0)
         transpose_x(2, 0, PAIR, nc.scalar.copy)
-        transpose_x(2, PAIR, PAIR, nc.scalar.copy)
+        transpose_adjacency(3)
+        symmetrise(2)
         symmetrise(3)
+        self_gain(PAIR, PACK)
+        transpose_x(2, PAIR, PAIR, nc.scalar.copy)
+        bias_onto_partitions()
         project_h1(1)
         bring_h0(1, 0)
         transpose_x(3, 0, PAIR, nc.scalar.copy)
@@ -390,33 +391,33 @@ def tile_modulatedgraphconv_pa_e_kernel(tc, x, W_words, W_scales, M, adj, adj2, 
         quantise_x(2)
         modulate(1, 1)
         weigh(0, PAIR)
-        weigh(1, 0)
         bring_h0(1, PAIR)
-        weigh(1, PAIR)
         aggregate_transposed(0)
         project_h1(2)
         quantise_x(3)
+        weigh(1, 0)
+        weigh(1, PAIR)
         modulate(2, 0)
         quantise_g(1)
         modulate(2, 1)
         bring_h0(2, 0)
         bring_h0(2, PAIR)
         weigh(2, 0)
-        weigh(2, PAIR)
         project_h1(3)
         aggregate_transposed(1)
         modulate(3, 0)
         quantise_g(2)
-        transpose_back(0)
         modulate(3, 1)
-        bring_h0(3, 0)
-        weigh(3, 0)
-        aggregate_transposed(2)
-        quantise_g(3)
+        weigh(2, PAIR)
+        transpose_back(0)
         finish(0, 0)
+        quantise_g(3)
         finish(0, PAIR)
         h0_on_vector(3, PAIR)
         weigh_on_vector(3, PAIR)
+        bring_h0(3, 0)
+        weigh(3, 0)
+        aggregate_transposed(2)
         transpose_back(1)
         finish(1, 0)
         finish(1, PAIR)

from contextlib import ExitStack

import concourse.mybir as mybir
from concourse.masks import make_identity

FP8X4 = mybir.dt.float8_e4m3fn_x4
BF16 = mybir.dt.bfloat16
F32 = mybir.dt.float32
I32 = mybir.dt.int32
U32 = mybir.dt.uint32
U8 = mybir.dt.uint8
ALU = mybir.AluOpType
ACT = mybir.ActivationFunctionType

P = 128
PACK = 4
BATCH, NODES, CIN, COUT = 4, 512, 512, 256
HALVES = COUT // P
BANK = 512
PAIR = BANK // COUT
QUADRANT = 32
SCALE_ROWS = QUADRANT // 8
SCALAR_RING, VECTOR_RING = 3, 5

FLOPS = 2 * BATCH * NODES * CIN * 2 * COUT + 2 * BATCH * NODES * NODES * COUT


def tile_modulatedgraphconv_pa_e_kernel(tc, x, W_words, W_scales, M, adj, adj2, bias, out):
    nc = tc.nc
    with ExitStack() as ctx:
        keep = ctx.enter_context(tc.tile_pool(name="keep", bufs=1))
        per_batch = ctx.enter_context(tc.tile_pool(name="per_batch", bufs=BATCH))
        psum = ctx.enter_context(tc.psum_pool(name="psum", bufs=1))

        def bank_for_scalar(shape, dtype=F32):
            return psum.tile(shape, dtype, name="bank_for_scalar", tag="for_scalar", bufs=SCALAR_RING)

        def bank_for_vector(shape):
            return psum.tile(shape, F32, name="bank_for_vector", tag="for_vector", bufs=VECTOR_RING)

        ctx.enter_context(tc.manual_schedule())

        warm = keep.tile([P, P], F32)
        nc.vector.memset(warm[:], 0.0)

        x_sb = [keep.tile([P, PACK, CIN], BF16, name="x_sb%d" % b) for b in range(BATCH)]
        w_words = keep.tile([P, 2 * COUT], U32, align_bytes=64)
        w_scales = keep.tile([P, 2 * COUT], U8, align_bytes=64)
        m_sb = keep.tile([P, PACK, COUT], BF16)
        diag_adj = keep.tile([P, PACK], BF16)
        diag_adj2 = keep.tile([P, PACK], BF16)
        adj_sb = keep.tile([P, PACK, NODES], BF16)
        adj2_sb = keep.tile([P, PACK, NODES], BF16)
        bias_rows = keep.tile([P, COUT], BF16)

        def load_x(b, piece):
            rows = x[b].rearrange("(t p) k -> p t k", t=PACK)
            for first_slot in range(0, PACK, piece):
                slots = slice(first_slot, first_slot + piece)
                nc.sync.dma_start(out=x_sb[b][:, slots, :], in_=rows[:, slots, :])

        def load_diagonal(dest, matrix):
            diagonal = matrix.rearrange("i j -> (i j)")[0 : NODES * NODES : NODES + 1]
            with nc.allow_non_contiguous_dma(reason="the diagonal of a matrix is 512 single elements"):
                nc.sync.dma_start(out=dest[:], in_=diagonal.rearrange("(t p) -> p t", t=PACK))

        load_x(0, PAIR)
        nc.sync.dma_start(
            out=w_words[:].bitcast(I32).rearrange("p (e n) -> p e n", e=2),
            in_=W_words.rearrange("e p n t -> p e (n t)").bitcast(I32),
        )
        nc.vector.memset(w_scales[:].bitcast(I32), 0)
        for quadrant in range(P // QUADRANT):
            live = slice(QUADRANT * quadrant, QUADRANT * quadrant + SCALE_ROWS)
            rows = slice(SCALE_ROWS * quadrant, SCALE_ROWS * (quadrant + 1))
            nc.sync.dma_start(
                out=w_scales[live, :].bitcast(I32).rearrange("r (e n) -> r e n", e=2),
                in_=W_scales[:, rows, :].rearrange("e r n -> r e n").bitcast(I32),
            )
        for first_slot in range(0, PACK, PAIR):
            slots = slice(first_slot, first_slot + PAIR)
            for tile, matrix in ((adj_sb, adj), (adj2_sb, adj2)):
                nc.sync.dma_start(out=tile[:, slots, :], in_=matrix.rearrange("(t p) i -> p t i", t=PACK)[:, slots, :])
        load_x(1, PACK)
        load_diagonal(diag_adj, adj)
        load_diagonal(diag_adj2, adj2)
        load_x(2, PACK)
        load_x(3, PACK)
        ident_f32 = keep.tile([P, P], F32)
        make_identity(nc, ident_f32[:])
        ident_bf16 = keep.tile([P, P], BF16)
        nc.vector.tensor_copy(out=ident_bf16[:], in_=ident_f32[:])
        ones = keep.tile([P, P], BF16)
        nc.vector.memset(ones[:], 1.0)
        flip_diagonal = keep.tile([P, PACK, P], F32)
        for r in range(PACK):
            nc.scalar.activation(out=flip_diagonal[:, r, :], in_=ident_f32[:], func=ACT.Copy, bias=1.0, scale=-2.0)

        nc.gpsimd.dma_start(out=m_sb[:], in_=M.rearrange("(t p) c -> p t c", t=PACK))
        nc.gpsimd.memset(bias_rows[:], 0.0)
        nc.gpsimd.dma_start(out=bias_rows[0:1, :], in_=bias.rearrange("(o c) -> o c", o=1))

        xq_words = keep.tile([P, BATCH, NODES], U32, align_bytes=64)
        xq_scales = keep.tile([P, BATCH, NODES], U8, align_bytes=64)
        g_words = keep.tile([P, BATCH, COUT], U32, align_bytes=64)
        g_scales = keep.tile([P, BATCH, COUT], U8, align_bytes=64)
        a_words = keep.tile([P, NODES], U32, align_bytes=64)
        a_scales = keep.tile([P, NODES], U8, align_bytes=64)

        x_grouped = {}

        def transpose_x(b, first_slot, slots, copy):
            if first_slot == 0:
                x_grouped[b] = per_batch.tile([P, NODES * PACK], BF16, name="x_grouped", align_bytes=64)
            x_pairs = x_sb[b][:].rearrange("p t k -> p (t k)").bitcast(F32)
            x_pairs = x_pairs.rearrange("p (t w u) -> p t w u", t=PACK, u=2)
            grouped_pairs = x_grouped[b][:].bitcast(F32).rearrange("p (s r u) -> p s r u", s=PACK, u=2)
            xt_ps = bank_for_scalar([P, slots, 2, P])
            for s in range(slots):
                for u in range(2):
                    nc.tensor.transpose(xt_ps[:, s, u, :], x_pairs[:, first_slot + s, :, u], ident_f32[:])
            copy(
                out=grouped_pairs[:, first_slot : first_slot + slots, :, :],
                in_=xt_ps[:].rearrange("p s u r -> p s r u"),
            )

        def quantise_x(b, first_slot=0, slots=PACK):
            nodes = slice(first_slot * P, (first_slot + slots) * P)
            nc.vector.quantize_mx(
                out=xq_words[:, b, nodes].bitcast(FP8X4),
                scales=xq_scales[:, b, nodes],
                in_=x_grouped[b][:, first_slot * P * PACK : (first_slot + slots) * P * PACK],
            )

        h1_banks = {}
        g_grouped = {}

        def project_h1(b):
            for h in range(HALVES):
                w1_cols = slice(COUT + h * P, COUT + (h + 1) * P)
                h1_banks[(b, h)] = bank_for_vector([P, PACK, P])
                for t in range(PACK):
                    nodes = slice(t * P, (t + 1) * P)
                    nc.tensor.matmul_mx(
                        out=h1_banks[(b, h)][:, t, :],
                        lhsT=xq_words[:, b, nodes].bitcast(FP8X4),
                        lhsT_scale=xq_scales[:, b, nodes],
                        rhs=w_words[:, w1_cols].bitcast(FP8X4),
                        rhs_scale=w_scales[:, w1_cols],
                        start=True,
                        stop=True,
                    )

        def modulate(b, h):
            if h == 0:
                g_grouped[b] = per_batch.tile([P, COUT, PACK], BF16, name="g_grouped", align_bytes=64)
            channels = slice(h * P, (h + 1) * P)
            nc.vector.tensor_tensor(
                out=g_grouped[b][:, channels, :],
                in0=h1_banks[(b, h)][:].rearrange("p t c -> p c t"),
                in1=m_sb[:, :, channels].rearrange("p t c -> p c t"),
                op=ALU.mult,
            )

        def quantise_g(b):
            nc.vector.quantize_mx(
                out=g_words[:, b, :].bitcast(FP8X4),
                scales=g_scales[:, b, :],
                in_=g_grouped[b][:].rearrange("p c t -> p (c t)"),
            )

        sums_run = keep.tile([P, PACK * (NODES + P)], F32)
        sums = sums_run[:, 0 : PACK * NODES].rearrange("p (r i) -> p r i", r=PACK)
        squares = sums_run[:].rearrange("p (r w) -> p r w", r=PACK)[:, :, 0:P]
        a_grouped = keep.tile([P, NODES, PACK], BF16, align_bytes=64)
        a_banks = {}

        def add_adjacency(r, engine):
            engine.tensor_tensor(out=sums[:, r, :], in0=adj_sb[:, r, :], in1=adj2_sb[:, r, :], op=ALU.add)

        def flip_the_diagonal():
            nc.gpsimd.tensor_tensor(out=squares, in0=squares, in1=flip_diagonal[:], op=ALU.mult)

        def transpose_adjacency(c):
            a_banks[c] = bank_for_vector([P, PACK, P])
            for t in range(PACK):
                columns = slice(t * P, (t + 1) * P)
                nc.tensor.matmul(out=a_banks[c][:, t, :], lhsT=adj_sb[:, c, columns], rhs=ident_bf16[:], start=True, stop=False)
                nc.tensor.matmul(out=a_banks[c][:, t, :], lhsT=adj2_sb[:, c, columns], rhs=ident_bf16[:], start=False, stop=True)

        def symmetrise(c):
            columns = slice(c * P, (c + 1) * P)
            nc.vector.tensor_tensor(
                out=a_grouped[:, columns, :],
                in0=a_banks[c][:].rearrange("p t q -> p q t"),
                in1=sums[:, :, columns].rearrange("p t q -> p q t"),
                op=ALU.add,
            )

        def quantise_a():
            nc.vector.quantize_mx(
                out=a_words[:].bitcast(FP8X4),
                scales=a_scales[:],
                in_=a_grouped[:].rearrange("p i t -> p (i t)"),
            )

        a_self = keep.tile([P, PACK], F32)
        gain = keep.tile([P, PACK, COUT], F32)
        h0_banks = {}
        self_term = {}

        def self_diagonal():
            nc.gpsimd.tensor_tensor(out=a_self[:], in0=diag_adj[:], in1=diag_adj2[:], op=ALU.add)

        def self_gain(first, last):
            for t in range(first, last):
                nc.scalar.activation(out=gain[:, t, :], in_=m_sb[:, t, :], func=ACT.Copy, scale=a_self[:, t : t + 1])

        def new_self_term(b):
            self_term[b] = per_batch.tile([P, PACK, COUT], F32, name="self_term")

        def project_h0(b, first_slot, bank):
            for s in range(PAIR):
                nodes = slice((first_slot + s) * P, (first_slot + s + 1) * P)
                nc.tensor.matmul_mx(
                    out=bank[:, s, :],
                    lhsT=xq_words[:, b, nodes].bitcast(FP8X4),
                    lhsT_scale=xq_scales[:, b, nodes],
                    rhs=w_words[:, 0:COUT].bitcast(FP8X4),
                    rhs_scale=w_scales[:, 0:COUT],
                    start=True,
                    stop=True,
                )

        def h0_on_vector(b, first_slot):
            h0_banks[(b, first_slot)] = bank_for_vector([P, PAIR, COUT])
            project_h0(b, first_slot, h0_banks[(b, first_slot)])

        def weigh_on_vector(b, first_slot):
            slots = slice(first_slot, first_slot + PAIR)
            nc.vector.tensor_tensor(
                out=self_term[b][:, slots, :], in0=h0_banks[(b, first_slot)][:], in1=gain[:, slots, :], op=ALU.mult
            )

        def bring_h0(b, first_slot):
            bank = bank_for_scalar([P, PAIR, COUT])
            project_h0(b, first_slot, bank)
            slots = slice(first_slot, first_slot + PAIR)
            nc.scalar.copy(out=self_term[b][:, slots, :], in_=bank[:])

        def weigh(b, first_slot):
            for t in range(first_slot, first_slot + PAIR):
                term = self_term[b][:, t, :]
                nc.gpsimd.tensor_tensor(out=term, in0=term, in1=gain[:, t, :], op=ALU.mult)

        bias_pair = keep.tile([P, PAIR, COUT], F32)
        bias_col = keep.tile([P, HALVES], F32)
        agg_t = {}
        agg_banks = {}

        def bias_onto_partitions():
            for h in range(HALVES):
                col_ps = bank_for_scalar([P, P], BF16)
                nc.tensor.transpose(col_ps[:], bias_rows[:, h * P : (h + 1) * P], ident_bf16[:])
                nc.scalar.copy(out=bias_col[:, h : h + 1], in_=col_ps[:, 0:1])

        def spread_bias():
            bias_ps = bank_for_scalar([P, HALVES, P])
            for h in range(HALVES):
                nc.tensor.transpose(bias_ps[:, h, :], bias_col[:, h : h + 1].to_broadcast([P, P]), ident_f32[:])
            for s in range(PAIR):
                nc.scalar.copy(out=bias_pair[:, s, :], in_=bias_ps[:].rearrange("p h c -> p (h c)"))

        def add_bias(b, first_slot):
            slots = slice(first_slot, first_slot + PAIR)
            nc.gpsimd.tensor_tensor(out=self_term[b][:, slots, :], in0=self_term[b][:, slots, :], in1=bias_pair[:], op=ALU.add)

        def aggregate(b):
            for first_slot in range(0, PACK, PAIR):
                bank = bank_for_vector([P, PAIR, COUT])
                agg_banks[(b, first_slot)] = bank
                for s in range(PAIR):
                    nodes = slice((first_slot + s) * P, (first_slot + s + 1) * P)
                    nc.tensor.matmul_mx(
                        out=bank[:, s, :],
                        lhsT=a_words[:, nodes].bitcast(FP8X4),
                        lhsT_scale=a_scales[:, nodes],
                        rhs=g_words[:, b, :].bitcast(FP8X4),
                        rhs_scale=g_scales[:, b, :],
                        start=True,
                        stop=True,
                    )

        def aggregate_transposed(b):
            agg_t[b] = per_batch.tile([P, HALVES, NODES], F32, name="agg_t")
            for h in range(HALVES):
                channels = slice(h * P, (h + 1) * P)
                agg_ps = bank_for_scalar([P, BANK])
                nc.tensor.matmul_mx(
                    out=agg_ps[:],
                    lhsT=g_words[:, b, channels].bitcast(FP8X4),
                    lhsT_scale=g_scales[:, b, channels],
                    rhs=a_words[:].bitcast(FP8X4),
                    rhs_scale=a_scales[:],
                    start=True,
                    stop=True,
                )
                nc.scalar.activation(
                    out=agg_t[b][:, h, :], in_=agg_ps[:], func=ACT.Identity, bias=bias_col[:, h : h + 1], scale=0.5
                )

        def transpose_back(b):
            for first_slot in range(0, PACK, PAIR):
                bank = bank_for_vector([P, PAIR, COUT])
                agg_banks[(b, first_slot)] = bank
                for s in range(PAIR):
                    nodes = slice((first_slot + s) * P, (first_slot + s + 1) * P)
                    for h in range(HALVES):
                        nc.tensor.transpose(bank[:, s, h * P : (h + 1) * P], agg_t[b][:, h, nodes], ident_f32[:])

        out_sb = {}

        def finish(b, first_slot):
            if first_slot == 0:
                out_sb[b] = per_batch.tile([P, PACK, COUT], F32, name="out_sb")
            slots = slice(first_slot, first_slot + PAIR)
            nc.vector.tensor_tensor(
                out=out_sb[b][:, slots, :], in0=agg_banks[(b, first_slot)][:], in1=self_term[b][:, slots, :], op=ALU.add
            )
            nc.sync.dma_start(out=out[b].rearrange("(t p) c -> p t c", t=PACK)[:, slots, :], in_=out_sb[b][:, slots, :])

        def warm_up(passes):
            warm_ps = bank_for_vector([P, P])
            for i in range(passes):
                nc.tensor.matmul(out=warm_ps[:], lhsT=warm[:], rhs=warm[:], start=True, stop=True)

        def keep_warm(passes):
            warm_ps = bank_for_vector([P, BANK])
            for i in range(passes):
                nc.tensor.matmul_mx(
                    out=warm_ps[:],
                    lhsT=w_words[:, 0:P].bitcast(FP8X4),
                    lhsT_scale=w_scales[:, 0:P],
                    rhs=w_words[:].bitcast(FP8X4),
                    rhs_scale=w_scales[:],
                    start=True,
                    stop=True,
                )

        for b in range(BATCH):
            new_self_term(b)
        warm_up(4)
        transpose_x(0, 0, PAIR, nc.scalar.copy)
        transpose_x(0, PAIR, PAIR, nc.vector.tensor_copy)
        warm_up(2)
        quantise_x(0, 0, PAIR)
        quantise_x(0, PAIR, PAIR)
        for r in range(PACK):
            add_adjacency(r, nc.vector)
        flip_the_diagonal()
        self_diagonal()
        transpose_adjacency(0)
        bring_h0(0, 0)
        bring_h0(0, PAIR)
        project_h1(0)
        transpose_adjacency(1)
        modulate(0, 0)
        modulate(0, 1)
        transpose_x(1, 0, PAIR, nc.scalar.copy)
        transpose_x(1, PAIR, PAIR, nc.scalar.copy)
        quantise_g(0)
        symmetrise(0)
        symmetrise(1)
        transpose_adjacency(2)
        quantise_x(1)
        self_gain(0, PAIR)
        weigh(0, 0)
        transpose_x(2, 0, PAIR, nc.scalar.copy)
        transpose_adjacency(3)
        symmetrise(2)
        symmetrise(3)
        self_gain(PAIR, PACK)
        transpose_x(2, PAIR, PAIR, nc.scalar.copy)
        bias_onto_partitions()
        project_h1(1)
        bring_h0(1, 0)
        transpose_x(3, 0, PAIR, nc.scalar.copy)
        transpose_x(3, PAIR, PAIR, nc.scalar.copy)
        modulate(1, 0)
        quantise_a()
        quantise_x(2)
        modulate(1, 1)
        weigh(0, PAIR)
        bring_h0(1, PAIR)
        aggregate_transposed(0)
        project_h1(2)
        quantise_x(3)
        weigh(1, 0)
        weigh(1, PAIR)
        modulate(2, 0)
        quantise_g(1)
        modulate(2, 1)
        bring_h0(2, 0)
        bring_h0(2, PAIR)
        weigh(2, 0)
        project_h1(3)
        aggregate_transposed(1)
        modulate(3, 0)
        quantise_g(2)
        modulate(3, 1)
        weigh(2, PAIR)
        transpose_back(0)
        finish(0, 0)
        quantise_g(3)
        finish(0, PAIR)
        h0_on_vector(3, PAIR)
        weigh_on_vector(3, PAIR)
        bring_h0(3, 0)
        weigh(3, 0)
        aggregate_transposed(2)
        transpose_back(1)
        finish(1, 0)
        finish(1, PAIR)
        aggregate_transposed(3)
        transpose_back(2)
        finish(2, 0)
        finish(2, PAIR)
        transpose_back(3)
        finish(3, 0)
        finish(3, PAIR)
